import numpy as np
import ml_dtypes


def mxq(x, axis, fmt="e4m3"):
    dtype, down = {"e4m3": (ml_dtypes.float8_e4m3fn, 7), "e5m2": (ml_dtypes.float8_e5m2, 14)}[fmt]
    v = np.moveaxis(np.asarray(x, np.float32).astype(ml_dtypes.bfloat16).astype(np.float64), axis, -1)
    blocks = v.reshape(v.shape[:-1] + (-1, 32))
    amax = np.abs(blocks).max(-1, keepdims=True)
    byte = np.maximum(np.where(amax > 0, np.frexp(amax)[1] - 1 + 127, 0) - down, 1)
    scale = np.exp2(byte - 127.0)
    codes = (blocks / scale).astype(np.float32).astype(dtype).astype(np.float64)
    return np.moveaxis((codes * scale).reshape(v.shape), -1, axis)


WIDE = False


def mx_kscale(k):
    if not WIDE:
        return np.ones(k)
    levels = np.array([10, -10, 5, -5, 0])
    if k % 512:
        return np.exp2(np.random.permutation(np.resize(levels, k // 32))).repeat(32)
    a = np.empty((k // 512, 16))
    for p in range(k // 512):
        a[p, :8] = np.random.permutation(np.resize(levels, 8))
        for g in range(8):
            far = levels[np.abs(levels - a[p, g]) >= 10]
            a[p, g + 8] = far[np.random.randint(len(far))]
    return np.exp2(a.ravel()).repeat(32)


BF16 = ml_dtypes.bfloat16


def bf(x):
    return np.asarray(x, np.float32).astype(BF16)


def f64(x):
    return np.asarray(x).astype(np.float64)


B, T, N, D, H, F = 1, 2048, 2, 2048, 16, 2048
S = B * N
EPS = 1e-5


def layernorm(v, g, b):
    mu = v.mean(-1, keepdims=True)
    var = np.square(v - mu).mean(-1, keepdims=True)
    return (v - mu) / np.sqrt(var + EPS) * g + b


def setup_inputs():
    s = mx_kscale(D)
    t = mx_kscale(D)
    return {"ax_cat": bf(np.random.standard_normal((S, T, D)) * 4.0 * s),
            "features": bf(np.random.standard_normal((B, T, N, D))),
            "wout_w": bf(np.random.standard_normal((D, D)) * 0.5 / np.sqrt(D) / s),
            "ln_g": bf((1.0 + 0.1 * np.random.standard_normal(D)) * t),
            "ln_b": bf(0.1 * np.random.standard_normal(D) * t),
            "ff1_w": bf(np.random.standard_normal((F, D)) / np.sqrt(D) / t),
            "ff1_b": bf(0.1 * np.random.standard_normal(F))}


def reference(ax_cat, features, wout_w, ln_g, ln_b, ff1_w, ff1_b):
    x = f64(features).transpose(0, 2, 1, 3).reshape(S, T, D)
    y = mxq(f64(ax_cat), 2, "e4m3") @ mxq(f64(wout_w), 1, "e4m3").T
    m = layernorm(y + x, f64(ln_g), f64(ln_b))
    return np.maximum((mxq(m, 2, "e4m3") @ mxq(f64(ff1_w), 1, "e4m3").T) + f64(ff1_b), 0.0)

@@ -1,0 +1,242 @@
+from contextlib import ExitStack
+
+import concourse.mybir as mybir
+from concourse.masks import make_identity
+
+F32 = mybir.dt.float32
+BF16 = mybir.dt.bfloat16
+U32 = mybir.dt.uint32
+U8 = mybir.dt.uint8
+FP8X4 = mybir.dt.float8_e4m3fn_x4
+ALU = mybir.AluOpType
+ACT = mybir.ActivationFunctionType
+
+P = 128
+D = 2048
+SEQ = 2
+T = 2048
+NT = SEQ * T // P
+KP = 4
+NB = 4
+EPS = 1e-5
+LZ = 2
+L2 = 3
+
+FLOPS = 2 * 2 * SEQ * T * D * D
+
+
+def tile_temporalatt_pb_l_kernel(tc, ax_cat, features, wout_w, ln_g, ln_b, ff1_w, ff1_b, out):
+    nc = tc.nc
+    with ExitStack() as ctx:
+        keep = ctx.enter_context(tc.tile_pool(name="keep", bufs=1))
+        work = ctx.enter_context(tc.tile_pool(name="work", bufs=2))
+        small = ctx.enter_context(tc.tile_pool(name="small", bufs=4))
+        tp_pool = ctx.enter_context(tc.psum_pool(name="tpp", bufs=4))
+        mm_pool = ctx.enter_context(tc.psum_pool(name="mmp", bufs=4))
+
+        eps_t = keep.tile([P, 1], F32, name="eps_t", tag="eps_t")
+        nc.vector.memset(eps_t[:], EPS)
+        warm = keep.tile([P, 1], F32, name="warm", tag="warm")
+        nc.scalar.activation(out=warm[:], in_=eps_t[:], func=ACT.Sqrt)
+
+        ident = keep.tile([P, P], F32, name="ident", tag="ident")
+        make_identity(nc, ident[:])
+
+        g_raw = keep.tile([P, 16], BF16, name="g_raw", tag="g_raw")
+        b_raw = keep.tile([P, 16], BF16, name="b_raw", tag="b_raw")
+        nc.sync.dma_start(out=g_raw[:].rearrange("p (g t) -> p g t", g=4, t=4),
+                          in_=ln_g.rearrange("(g p t) -> p g t", g=4, p=P, t=4))
+        nc.sync.dma_start(out=b_raw[:].rearrange("p (g t) -> p g t", g=4, t=4),
+                          in_=ln_b.rearrange("(g p t) -> p g t", g=4, p=P, t=4))
+        g_col = keep.tile([P, 16], F32, name="g_col", tag="g_col")
+        b_col = keep.tile([P, 16], F32, name="b_col", tag="b_col")
+        nc.vector.tensor_copy(out=g_col[:], in_=g_raw[:])
+        nc.vector.tensor_copy(out=b_col[:], in_=b_raw[:])
+
+        w1q = keep.tile([P, KP, D], U32, name="w1q", tag="w1q", align_bytes=64)
+        w1s = keep.tile([P, KP, D], U8, name="w1s", tag="w1s", align_bytes=64)
+        w2q = keep.tile([P, KP, D], U32, name="w2q", tag="w2q", align_bytes=64)
+        w2s = keep.tile([P, KP, D], U8, name="w2s", tag="w2s", align_bytes=64)
+        fb = keep.tile([P, D], BF16, name="fb", tag="fb")
+
+        def load_rows(rows):
+            raw = work.tile([P, D], BF16, name="raw", tag="raw", bufs=4)
+            nc.sync.dma_start(out=raw[:], in_=rows)
+            return raw
+
+        def copy_on(engine_is_scalar, dst, src):
+            if engine_is_scalar:
+                nc.scalar.copy(out=dst, in_=src)
+            else:
+                nc.vector.tensor_copy(out=dst, in_=src)
+
+        def words_to_k(words_of, evac_scalar):
+            grp = work.tile([P, D], BF16, name="grp", tag="grp", bufs=3, align_bytes=64)
+            grp_w = grp[:].bitcast(F32).rearrange("p (g r u) -> p g r u", g=KP, r=P, u=2)
+            for h in range(2):
+                bank = tp_pool.tile([P, 512], F32, name="tpb", tag="tpb")
+                for g2 in range(2):
+                    for u in range(2):
+                        c0 = (2 * g2 + u) * P
+                        nc.tensor.transpose(bank[:, c0:c0 + P], words_of(2 * h + g2, u), ident[:])
+                copy_on(evac_scalar[h], grp_w[:, 2 * h:2 * h + 2],
+                        bank[:].rearrange("p (g u r) -> p g r u", g=2, u=2, r=P))
+            return grp
+
+        def prep_weight(rows, wq, ws, col0, idx):
+            raw = load_rows(rows)
+            raw_w = raw[:].bitcast(F32)
+            grp = words_to_k(lambda g, u: raw_w[:, 256 * g + u:256 * (g + 1):2],
+                             (idx % 2 == 0, idx % 2 == 1))
+            for kp in range(KP):
+                nc.vector.quantize_mx(out=wq[:, kp, col0:col0 + P].bitcast(FP8X4),
+                                      scales=ws[:, kp, col0:col0 + P],
+                                      in_=grp[:, 512 * kp:512 * (kp + 1)])
+
+        def tok(i):
+            return i // (T // P), (i % (T // P)) * P
+
+        raws = {}
+        srts = {}
+        xs = {}
+        axqs = {}
+        rs = {}
+        sums_d = {}
+        zs = {}
+        mqs = {}
+
+        def load_ax(i):
+            s, t0 = tok(i)
+            raws[i] = load_rows(ax_cat[s, t0:t0 + P, :])
+
+        def load_x(i):
+            s, t0 = tok(i)
+            x = work.tile([P, D], BF16, name="x", tag="x", bufs=3)
+            nc.sync.dma_start(out=x[:], in_=features[0, t0:t0 + P, s, :])
+            xs[i] = x
+
+        def sort_ax(i):
+            raw = raws.pop(i)
+            srt = work.tile([P, D], BF16, name="srt", tag="srt", bufs=2)
+            nc.scalar.copy(out=srt[:].bitcast(F32).rearrange("p (g u w) -> p g u w", g=KP, u=2, w=P),
+                           in_=raw[:].bitcast(F32).rearrange("p (g w u) -> p g u w", g=KP, w=P, u=2))
+            srts[i] = srt
+
+        def prep_ax(i):
+            srt_w = srts.pop(i)[:].bitcast(F32)
+            grp = words_to_k(lambda g, u: srt_w[:, (2 * g + u) * P:(2 * g + u + 1) * P], (True, False))
+            q = work.tile([P, KP * P], U32, name="axq", tag="axq", bufs=2, align_bytes=64)
+            sc = work.tile([P, KP * P], U8, name="axs", tag="axs", bufs=2, align_bytes=64)
+            nc.vector.quantize_mx(out=q[:].bitcast(FP8X4), scales=sc[:], in_=grp[:])
+            axqs[i] = (q, sc)
+
+        def mx_group(ps, q, sc, wq, ws, b):
+            for kp in range(KP):
+                nc.tensor.matmul_mx(out=ps[:],
+                                    lhsT=q[:, kp * P:(kp + 1) * P].bitcast(FP8X4),
+                                    lhsT_scale=sc[:, kp * P:(kp + 1) * P],
+                                    rhs=wq[:, kp, 512 * b:512 * (b + 1)].bitcast(FP8X4),
+                                    rhs_scale=ws[:, kp, 512 * b:512 * (b + 1)],
+                                    start=(kp == 0), stop=(kp == KP - 1))
+
+        def stage1(i):
+            q, sc = axqs.pop(i)
+            x = xs.pop(i)
+            xv = x[:].rearrange("p (v t) -> p t v", t=4)
+            r = work.tile([P, D], F32, name="r", tag="r", bufs=2)
+            sums = small.tile([P, NB], F32, name="sums", tag="sums")
+            for t in range(NB):
+                ps = mm_pool.tile([P, 512], F32, name="mmb", tag="mmb")
+                mx_group(ps, q, sc, w1q, w1s, t)
+                nc.vector.scalar_tensor_tensor(out=r[:, 512 * t:512 * (t + 1)], in0=ps[:], scalar=0.0,
+                                               in1=xv[:, t, :], op0=ALU.add, op1=ALU.add,
+                                               accum_out=sums[:, t:t + 1])
+            rs[i] = r
+            sums_d[i] = sums
+
+        def norm(i):
+            r = rs.pop(i)
+            sums = sums_d.pop(i)
+            junk4 = small.tile([P, NB], F32, name="junk4", tag="junk4")
+            negmu = small.tile([P, 1], F32, name="negmu", tag="negmu")
+            nc.scalar.activation(out=junk4[:], in_=sums[:], func=ACT.Copy, scale=-1.0 / D, accum_out=negmu[:])
+            junk = work.tile([P, D], BF16, name="junk", tag="junk", bufs=1)
+            ssq = small.tile([P, 1], F32, name="ssq", tag="ssq")
+            nc.scalar.activation(out=junk[:], in_=r[:], func=ACT.Square, bias=negmu[:], scale=1.0,
+                                 accum_out=ssq[:])
+            std = small.tile([P, 1], F32, name="std", tag="std")
+            nc.scalar.activation(out=std[:], in_=ssq[:], func=ACT.Sqrt, bias=eps_t[:], scale=1.0 / D)
+            rstd = small.tile([P, 1], F32, name="rstd", tag="rstd")
+            nc.vector.reciprocal(out=rstd[:], in_=std[:])
+            z = work.tile([P, D], F32, name="z", tag="z", bufs=2)
+            nc.vector.tensor_scalar(out=z[:], in0=r[:], scalar1=negmu[:], scalar2=rstd[:],
+                                    op0=ALU.add, op1=ALU.mult)
+            zs[i] = z
+
+        def prep_m(i):
+            z = zs.pop(i)
+            mt = work.tile([P, D], BF16, name="mt", tag="mt", bufs=2)
+            for g in range(KP):
+                bank = tp_pool.tile([P, 512], F32, name="tpb", tag="tpb")
+                for t in range(4):
+                    nc.tensor.transpose(bank[:, t * P:(t + 1) * P],
+                                        z[:, 512 * t + P * g:512 * t + P * (g + 1)], ident[:])
+                for t in range(4):
+                    c = 4 * g + t
+                    nc.scalar.activation(out=mt[:, c * P:(c + 1) * P], in_=bank[:, t * P:(t + 1) * P],
+                                         func=ACT.Identity, scale=g_col[:, c:c + 1], bias=b_col[:, c:c + 1])
+            grp = work.tile([P, D], BF16, name="grp", tag="grp", bufs=3, align_bytes=64)
+            nc.vector.tensor_copy(out=grp[:].rearrange("p (g c t) -> p g c t", g=KP, c=P, t=4),
+                                  in_=mt[:].rearrange("p (g t c) -> p g c t", g=KP, t=4, c=P))
+            q = work.tile([P, KP * P], U32, name="mq", tag="mq", bufs=3, align_bytes=64)
+            sc = work.tile([P, KP * P], U8, name="ms", tag="ms", bufs=3, align_bytes=64)
+            nc.vector.quantize_mx(out=q[:].bitcast(FP8X4), scales=sc[:], in_=grp[:])
+            mqs[i] = (q, sc)
+
+        def stage2(i):
+            q, sc = mqs.pop(i)
+            s, t0 = tok(i)
+            o = work.tile([P, D], F32, name="o", tag="o", bufs=3)
+            for b in range(NB):
+                ps = mm_pool.tile([P, 512], F32, name="mmb", tag="mmb")
+                mx_group(ps, q, sc, w2q, w2s, b)
+                nc.vector.tensor_tensor(out=o[:, 512 * b:512 * (b + 1)], in0=ps[:],
+                                        in1=fb[:, 512 * b:512 * (b + 1)], op=ALU.add)
+                if b % 2 == 1:
+                    lo, hi = 512 * (b - 1), 512 * (b + 1)
+                    nc.scalar.activation(out=o[:, lo:hi], in_=o[:, lo:hi], func=ACT.Relu)
+                    nc.scalar.dma_start(out=out[s, t0:t0 + P, lo:hi], in_=o[:, lo:hi])
+
+        w1_rows = wout_w.rearrange("(g p t) k -> g t p k", g=4, p=P, t=4)
+        idx = 0
+        for t in range(4):
+            for g in range(4):
+                prep_weight(w1_rows[g, t], w1q, w1s, 512 * t + P * g, idx)
+                idx += 1
+        load_ax(0)
+        load_x(0)
+        load_ax(1)
+        for rt in range(16):
+            prep_weight(ff1_w[rt * P:(rt + 1) * P, :], w2q, w2s, rt * P, idx)
+            idx += 1
+        nc.sync.dma_start(out=fb[:], in_=ff1_b.partition_broadcast(P))
+        sort_ax(0)
+        prep_ax(0)
+        sort_ax(1)
+
+        for j in range(NT + L2):
+            if j + 2 < NT:
+                load_ax(j + 2)
+            if j + 1 < NT:
+                load_x(j + 1)
+                prep_ax(j + 1)
+            if 0 <= j - LZ < NT:
+                prep_m(j - LZ)
+            if j < NT:
+                stage1(j)
+            if j + 2 < NT:
+                sort_ax(j + 2)
+            if 0 <= j - L2 < NT:
+                stage2(j - L2)
+            if j < NT:
+                norm(j)

@@ -21,6 +21,7 @@ NB = 4
 EPS = 1e-5
 LZ = 2
 L2 = 3
+W2_SPLIT = (6, 5, 5)
 
 FLOPS = 2 * 2 * SEQ * T * D * D
 
@@ -41,96 +42,132 @@ def tile_temporalatt_pb_l_kernel(tc, ax_cat, features, wout_w, ln_g, ln_b, ff1_w
 
         ident = keep.tile([P, P], F32, name="ident", tag="ident")
         make_identity(nc, ident[:])
-
-        g_raw = keep.tile([P, 16], BF16, name="g_raw", tag="g_raw")
-        b_raw = keep.tile([P, 16], BF16, name="b_raw", tag="b_raw")
-        nc.sync.dma_start(out=g_raw[:].rearrange("p (g t) -> p g t", g=4, t=4),
-                          in_=ln_g.rearrange("(g p t) -> p g t", g=4, p=P, t=4))
-        nc.sync.dma_start(out=b_raw[:].rearrange("p (g t) -> p g t", g=4, t=4),
-                          in_=ln_b.rearrange("(g p t) -> p g t", g=4, p=P, t=4))
-        g_col = keep.tile([P, 16], F32, name="g_col", tag="g_col")
-        b_col = keep.tile([P, 16], F32, name="b_col", tag="b_col")
-        nc.vector.tensor_copy(out=g_col[:], in_=g_raw[:])
-        nc.vector.tensor_copy(out=b_col[:], in_=b_raw[:])
+        ctx.enter_context(tc.manual_schedule())
 
         w1q = keep.tile([P, KP, D], U32, name="w1q", tag="w1q", align_bytes=64)
         w1s = keep.tile([P, KP, D], U8, name="w1s", tag="w1s", align_bytes=64)
         w2q = keep.tile([P, KP, D], U32, name="w2q", tag="w2q", align_bytes=64)
         w2s = keep.tile([P, KP, D], U8, name="w2s", tag="w2s", align_bytes=64)
         fb = keep.tile([P, D], BF16, name="fb", tag="fb")
+        g_raw = keep.tile([P, 16], BF16, name="g_raw", tag="g_raw")
+        b_raw = keep.tile([P, 16], BF16, name="b_raw", tag="b_raw")
+        g_col = keep.tile([P, 16], F32, name="g_col", tag="g_col")
+        b_col = keep.tile([P, 16], F32, name="b_col", tag="b_col")
+
+        def tok(i):
+            return i // (T // P), (i % (T // P)) * P
 
         def load_rows(rows):
             raw = work.tile([P, D], BF16, name="raw", tag="raw", bufs=4)
             nc.sync.dma_start(out=raw[:], in_=rows)
             return raw
 
-        def copy_on(engine_is_scalar, dst, src):
-            if engine_is_scalar:
+        def new_grp():
+            grp = work.tile([P, D], BF16, name="grp", tag="grp", bufs=3, align_bytes=64)
+            return grp
+
+        def word_transposes(words_of, h):
+            bank = tp_pool.tile([P, 512], F32, name="tpb", tag="tpb")
+            for g2 in range(2):
+                for u in range(2):
+                    c0 = (2 * g2 + u) * P
+                    nc.tensor.transpose(bank[:, c0:c0 + P], words_of(2 * h + g2, u), ident[:])
+            return bank
+
+        def word_evac(on_scalar, grp, bank, h):
+            dst = grp[:].bitcast(F32).rearrange("p (g r u) -> p g r u", g=KP, r=P, u=2)[:, 2 * h:2 * h + 2]
+            src = bank[:].rearrange("p (g u r) -> p g r u", g=2, u=2, r=P)
+            if on_scalar:
                 nc.scalar.copy(out=dst, in_=src)
             else:
                 nc.vector.tensor_copy(out=dst, in_=src)
 
-        def words_to_k(words_of, evac_scalar):
-            grp = work.tile([P, D], BF16, name="grp", tag="grp", bufs=3, align_bytes=64)
-            grp_w = grp[:].bitcast(F32).rearrange("p (g r u) -> p g r u", g=KP, r=P, u=2)
-            for h in range(2):
-                bank = tp_pool.tile([P, 512], F32, name="tpb", tag="tpb")
-                for g2 in range(2):
-                    for u in range(2):
-                        c0 = (2 * g2 + u) * P
-                        nc.tensor.transpose(bank[:, c0:c0 + P], words_of(2 * h + g2, u), ident[:])
-                copy_on(evac_scalar[h], grp_w[:, 2 * h:2 * h + 2],
-                        bank[:].rearrange("p (g u r) -> p g r u", g=2, u=2, r=P))
-            return grp
+        w1_rows = wout_w.rearrange("(g p t) k -> g t p k", g=4, p=P, t=4)
+        w_units = []
+        for t in range(4):
+            for g in range(4):
+                w_units.append((w1_rows[g, t], w1q, w1s, 512 * t + P * g))
+        for rt in range(16):
+            w_units.append((ff1_w[rt * P:(rt + 1) * P, :], w2q, w2s, rt * P))
+        w_raw = {}
+        w_grp = {}
 
-        def prep_weight(rows, wq, ws, col0, idx):
-            raw = load_rows(rows)
-            raw_w = raw[:].bitcast(F32)
-            grp = words_to_k(lambda g, u: raw_w[:, 256 * g + u:256 * (g + 1):2],
-                             (idx % 2 == 0, idx % 2 == 1))
+        def w_load(n):
+            w_raw[n] = load_rows(w_units[n][0])
+
+        def w_transpose(n):
+            raw_w = w_raw.pop(n)[:].bitcast(F32)
+            grp = new_grp()
+            for h in range(2):
+                bank = word_transposes(lambda g, u: raw_w[:, 256 * g + u:256 * (g + 1):2], h)
+                word_evac(h == 0, grp, bank, h)
+            w_grp[n] = grp
+
+        def w_quantize(n):
+            grp = w_grp.pop(n)
+            wq, ws, col0 = w_units[n][1], w_units[n][2], w_units[n][3]
             for kp in range(KP):
                 nc.vector.quantize_mx(out=wq[:, kp, col0:col0 + P].bitcast(FP8X4),
                                       scales=ws[:, kp, col0:col0 + P],
                                       in_=grp[:, 512 * kp:512 * (kp + 1)])
 
-        def tok(i):
-            return i // (T // P), (i % (T // P)) * P
-
         raws = {}
         srts = {}
         xs = {}
+        axg = {}
+        axb = {}
         axqs = {}
         rs = {}
         sums_d = {}
+        stat = {}
         zs = {}
+        mts = {}
+        mgrp = {}
         mqs = {}
+        os_d = {}
 
         def load_ax(i):
-            s, t0 = tok(i)
-            raws[i] = load_rows(ax_cat[s, t0:t0 + P, :])
+            if i < NT:
+                s, t0 = tok(i)
+                raw = work.tile([P, D], BF16, name="axraw", tag="axraw", bufs=3)
+                nc.sync.dma_start(out=raw[:], in_=ax_cat[s, t0:t0 + P, :])
+                raws[i] = raw
 
         def load_x(i):
-            s, t0 = tok(i)
-            x = work.tile([P, D], BF16, name="x", tag="x", bufs=3)
-            nc.sync.dma_start(out=x[:], in_=features[0, t0:t0 + P, s, :])
-            xs[i] = x
+            if i < NT:
+                s, t0 = tok(i)
+                x = work.tile([P, D], BF16, name="x", tag="x", bufs=3)
+                nc.sync.dma_start(out=x[:], in_=features[0, t0:t0 + P, s, :])
+                xs[i] = x
 
         def sort_ax(i):
-            raw = raws.pop(i)
-            srt = work.tile([P, D], BF16, name="srt", tag="srt", bufs=2)
-            nc.scalar.copy(out=srt[:].bitcast(F32).rearrange("p (g u w) -> p g u w", g=KP, u=2, w=P),
-                           in_=raw[:].bitcast(F32).rearrange("p (g w u) -> p g u w", g=KP, w=P, u=2))
-            srts[i] = srt
+            if i < NT:
+                raw = raws.pop(i)
+                srt = work.tile([P, D], BF16, name="srt", tag="srt", bufs=2)
+                nc.scalar.copy(out=srt[:].bitcast(F32).rearrange("p (g u w) -> p g u w", g=KP, u=2, w=P),
+                               in_=raw[:].bitcast(F32).rearrange("p (g w u) -> p g u w", g=KP, w=P, u=2))
+                srts[i] = srt
 
-        def prep_ax(i):
+        def ax_transposes(i):
             srt_w = srts.pop(i)[:].bitcast(F32)
-            grp = words_to_k(lambda g, u: srt_w[:, (2 * g + u) * P:(2 * g + u + 1) * P], (True, False))
+            axg[i] = new_grp()
+            axb[i] = []
+            for h in range(2):
+                axb[i].append(word_transposes(lambda g, u: srt_w[:, (2 * g + u) * P:(2 * g + u + 1) * P], h))
+
+        def ax_evac(i, h):
+            word_evac(h == 0, axg[i], axb[i][h], h)
+
+        def ax_quantize(i):
+            grp = axg.pop(i)
+            axb.pop(i)
             q = work.tile([P, KP * P], U32, name="axq", tag="axq", bufs=2, align_bytes=64)
             sc = work.tile([P, KP * P], U8, name="axs", tag="axs", bufs=2, align_bytes=64)
             nc.vector.quantize_mx(out=q[:].bitcast(FP8X4), scales=sc[:], in_=grp[:])
             axqs[i] = (q, sc)
 
-        def mx_group(ps, q, sc, wq, ws, b):
+        def mx_group(q, sc, wq, ws, b):
+            ps = mm_pool.tile([P, 512], F32, name="mmb", tag="mmb")
             for kp in range(KP):
                 nc.tensor.matmul_mx(out=ps[:],
                                     lhsT=q[:, kp * P:(kp + 1) * P].bitcast(FP8X4),
@@ -138,24 +175,26 @@ def tile_temporalatt_pb_l_kernel(tc, ax_cat, features, wout_w, ln_g, ln_b, ff1_w
                                     rhs=wq[:, kp, 512 * b:512 * (b + 1)].bitcast(FP8X4),
                                     rhs_scale=ws[:, kp, 512 * b:512 * (b + 1)],
                                     start=(kp == 0), stop=(kp == KP - 1))
+            return ps
 
-        def stage1(i):
-            q, sc = axqs.pop(i)
-            x = xs.pop(i)
-            xv = x[:].rearrange("p (v t) -> p t v", t=4)
-            r = work.tile([P, D], F32, name="r", tag="r", bufs=2)
-            sums = small.tile([P, NB], F32, name="sums", tag="sums")
-            for t in range(NB):
-                ps = mm_pool.tile([P, 512], F32, name="mmb", tag="mmb")
-                mx_group(ps, q, sc, w1q, w1s, t)
-                nc.vector.scalar_tensor_tensor(out=r[:, 512 * t:512 * (t + 1)], in0=ps[:], scalar=0.0,
-                                               in1=xv[:, t, :], op0=ALU.add, op1=ALU.add,
-                                               accum_out=sums[:, t:t + 1])
-            rs[i] = r
-            sums_d[i] = sums
+        def stage1_bank(i, t):
+            if t == 0:
+                r_new = work.tile([P, D], F32, name="r", tag="r", bufs=2)
+                sums_new = small.tile([P, NB], F32, name="sums", tag="sums")
+                rs[i] = r_new
+                sums_d[i] = sums_new
+            q, sc = axqs[i]
+            ps = mx_group(q, sc, w1q, w1s, t)
+            xv = xs[i][:].rearrange("p (v t) -> p t v", t=4)
+            nc.vector.scalar_tensor_tensor(out=rs[i][:, 512 * t:512 * (t + 1)], in0=ps[:], scalar=0.0,
+                                           in1=xv[:, t, :], op0=ALU.add, op1=ALU.add,
+                                           accum_out=sums_d[i][:, t:t + 1])
+            if t == NB - 1:
+                axqs.pop(i)
+                xs.pop(i)
 
-        def norm(i):
-            r = rs.pop(i)
+        def stats(i):
+            r = rs[i]
             sums = sums_d.pop(i)
             junk4 = small.tile([P, NB], F32, name="junk4", tag="junk4")
             negmu = small.tile([P, 1], F32, name="negmu", tag="negmu")
@@ -166,77 +205,185 @@ def tile_temporalatt_pb_l_kernel(tc, ax_cat, features, wout_w, ln_g, ln_b, ff1_w
                                  accum_out=ssq[:])
             std = small.tile([P, 1], F32, name="std", tag="std")
             nc.scalar.activation(out=std[:], in_=ssq[:], func=ACT.Sqrt, bias=eps_t[:], scale=1.0 / D)
-            rstd = small.tile([P, 1], F32, name="rstd", tag="rstd")
-            nc.vector.reciprocal(out=rstd[:], in_=std[:])
-            z = work.tile([P, D], F32, name="z", tag="z", bufs=2)
-            nc.vector.tensor_scalar(out=z[:], in0=r[:], scalar1=negmu[:], scalar2=rstd[:],
-                                    op0=ALU.add, op1=ALU.mult)
-            zs[i] = z
+            stat[i] = (negmu, std)
 
-        def prep_m(i):
-            z = zs.pop(i)
-            mt = work.tile([P, D], BF16, name="mt", tag="mt", bufs=2)
-            for g in range(KP):
-                bank = tp_pool.tile([P, 512], F32, name="tpb", tag="tpb")
-                for t in range(4):
-                    nc.tensor.transpose(bank[:, t * P:(t + 1) * P],
-                                        z[:, 512 * t + P * g:512 * t + P * (g + 1)], ident[:])
-                for t in range(4):
-                    c = 4 * g + t
-                    nc.scalar.activation(out=mt[:, c * P:(c + 1) * P], in_=bank[:, t * P:(t + 1) * P],
-                                         func=ACT.Identity, scale=g_col[:, c:c + 1], bias=b_col[:, c:c + 1])
-            grp = work.tile([P, D], BF16, name="grp", tag="grp", bufs=3, align_bytes=64)
-            nc.vector.tensor_copy(out=grp[:].rearrange("p (g c t) -> p g c t", g=KP, c=P, t=4),
-                                  in_=mt[:].rearrange("p (g t c) -> p g c t", g=KP, t=4, c=P))
-            q = work.tile([P, KP * P], U32, name="mq", tag="mq", bufs=3, align_bytes=64)
-            sc = work.tile([P, KP * P], U8, name="ms", tag="ms", bufs=3, align_bytes=64)
+        def z_half(i, h):
+            if h == 0:
+                negmu, std = stat[i]
+                rstd = small.tile([P, 1], F32, name="rstd", tag="rstd")
+                nc.vector.reciprocal(out=rstd[:], in_=std[:])
+                z_new = work.tile([P, D], F32, name="z", tag="z", bufs=2)
+                zs[i] = z_new
+                stat[i] = (negmu, rstd)
+            negmu, rstd = stat[i]
+            lo, hi = 1024 * h, 1024 * (h + 1)
+            nc.vector.tensor_scalar(out=zs[i][:, lo:hi], in0=rs[i][:, lo:hi], scalar1=negmu[:], scalar2=rstd[:],
+                                    op0=ALU.add, op1=ALU.mult)
+            if h == 1:
+                stat.pop(i)
+                rs.pop(i)
+
+        zb = {}
+
+        def z_transposes(i, g):
+            z = zs[i]
+            bank = tp_pool.tile([P, 512], F32, name="tpb", tag="tpb")
+            for t in range(4):
+                nc.tensor.transpose(bank[:, t * P:(t + 1) * P],
+                                    z[:, 512 * t + P * g:512 * t + P * (g + 1)], ident[:])
+            zb[(i, g)] = bank
+            if g == KP - 1:
+                zs.pop(i)
+
+        def m_evac(i, g):
+            if g == 0:
+                mt_new = work.tile([P, D], BF16, name="mt", tag="mt", bufs=2)
+                mts[i] = mt_new
+            bank = zb.pop((i, g))
+            for t in range(4):
+                c = 4 * g + t
+                nc.scalar.activation(out=mts[i][:, c * P:(c + 1) * P], in_=bank[:, t * P:(t + 1) * P],
+                                     func=ACT.Identity, scale=g_col[:, c:c + 1], bias=b_col[:, c:c + 1])
+
+        def m_interleave(i, h):
+            if h == 0:
+                mgrp[i] = new_grp()
+            lo, hi = 1024 * h, 1024 * (h + 1)
+            nc.vector.tensor_copy(out=mgrp[i][:, lo:hi].rearrange("p (g c t) -> p g c t", g=2, c=P, t=4),
+                                  in_=mts[i][:, lo:hi].rearrange("p (g t c) -> p g c t", g=2, t=4, c=P))
+            if h == 1:
+                mts.pop(i)
+
+        def m_quantize(i):
+            grp = mgrp.pop(i)
+            q = work.tile([P, KP * P], U32, name="mq", tag="mq", bufs=2, align_bytes=64)
+            sc = work.tile([P, KP * P], U8, name="ms", tag="ms", bufs=2, align_bytes=64)
             nc.vector.quantize_mx(out=q[:].bitcast(FP8X4), scales=sc[:], in_=grp[:])
             mqs[i] = (q, sc)
 
-        def stage2(i):
-            q, sc = mqs.pop(i)
+        def stage2_bank(i, b):
+            if b == 0:
+                o_new = work.tile([P, D], F32, name="o", tag="o", bufs=3)
+                os_d[i] = o_new
+            q, sc = mqs[i]
+            ps = mx_group(q, sc, w2q, w2s, b)
+            nc.vector.tensor_tensor(out=os_d[i][:, 512 * b:512 * (b + 1)], in0=ps[:],
+                                    in1=fb[:, 512 * b:512 * (b + 1)], op=ALU.add)
+            if b == NB - 1:
+                mqs.pop(i)
+
+        def relu_store(i, h):
             s, t0 = tok(i)
-            o = work.tile([P, D], F32, name="o", tag="o", bufs=3)
-            for b in range(NB):
-                ps = mm_pool.tile([P, 512], F32, name="mmb", tag="mmb")
-                mx_group(ps, q, sc, w2q, w2s, b)
-                nc.vector.tensor_tensor(out=o[:, 512 * b:512 * (b + 1)], in0=ps[:],
-                                        in1=fb[:, 512 * b:512 * (b + 1)], op=ALU.add)
-                if b % 2 == 1:
-                    lo, hi = 512 * (b - 1), 512 * (b + 1)
-                    nc.scalar.activation(out=o[:, lo:hi], in_=o[:, lo:hi], func=ACT.Relu)
-                    nc.scalar.dma_start(out=out[s, t0:t0 + P, lo:hi], in_=o[:, lo:hi])
+            o = os_d[i]
+            lo, hi = 1024 * h, 1024 * (h + 1)
+            nc.scalar.activation(out=o[:, lo:hi], in_=o[:, lo:hi], func=ACT.Relu)
+            nc.scalar.dma_start(out=out[s, t0:t0 + P, lo:hi], in_=o[:, lo:hi])
+            if h == 1:
+                os_d.pop(i)
 
-        w1_rows = wout_w.rearrange("(g p t) k -> g t p k", g=4, p=P, t=4)
-        idx = 0
-        for t in range(4):
-            for g in range(4):
-                prep_weight(w1_rows[g, t], w1q, w1s, 512 * t + P * g, idx)
-                idx += 1
         load_ax(0)
-        load_x(0)
-        load_ax(1)
-        for rt in range(16):
-            prep_weight(ff1_w[rt * P:(rt + 1) * P, :], w2q, w2s, rt * P, idx)
-            idx += 1
-        nc.sync.dma_start(out=fb[:], in_=ff1_b.partition_broadcast(P))
+        nc.sync.dma_start(out=g_raw[:].rearrange("p (g t) -> p g t", g=4, t=4),
+                          in_=ln_g.rearrange("(g p t) -> p g t", g=4, p=P, t=4))
+        nc.sync.dma_start(out=b_raw[:].rearrange("p (g t) -> p g t", g=4, t=4),
+                          in_=ln_b.rearrange("(g p t) -> p g t", g=4, p=P, t=4))
+        w_load(0)
+        w_load(1)
+        w_load(2)
+        nc.vector.tensor_copy(out=g_col[:], in_=g_raw[:])
+        nc.vector.tensor_copy(out=b_col[:], in_=b_raw[:])
         sort_ax(0)
-        prep_ax(0)
+        ax_transposes(0)
+        ax_evac(0, 0)
+        ax_evac(0, 1)
+        for n in range(16):
+            if n + 3 < 16:
+                w_load(n + 3)
+            if n == 8:
+                load_x(0)
+            if n == 10:
+                load_ax(1)
+            if n == 12:
+                load_x(1)
+            if n == 13:
+                load_ax(2)
+            w_transpose(n)
+            if n == 0:
+                ax_quantize(0)
+            else:
+                w_quantize(n - 1)
+        w_load(16)
+        w_load(17)
         sort_ax(1)
+        w_quantize(15)
+        w_next = 16
+        w_loaded = 18
 
+        carried = []
         for j in range(NT + L2):
-            if j + 2 < NT:
-                load_ax(j + 2)
+            i1, iz, i2 = j, j - LZ, j - L2
+            load_ax(j + 3)
+            load_x(j + 2)
             if j + 1 < NT:
-                load_x(j + 1)
-                prep_ax(j + 1)
-            if 0 <= j - LZ < NT:
-                prep_m(j - LZ)
-            if j < NT:
-                stage1(j)
-            if j + 2 < NT:
-                sort_ax(j + 2)
-            if 0 <= j - L2 < NT:
-                stage2(j - L2)
-            if j < NT:
-                norm(j)
+                ax_transposes(j + 1)
+            if 0 <= iz < NT:
+                z_transposes(iz, 0)
+                z_transposes(iz, 1)
+            if j + 1 < NT:
+                ax_evac(j + 1, 0)
+                ax_evac(j + 1, 1)
+            for i_old in carried:
+                relu_store(i_old, 1)
+            carried = []
+            if 0 <= iz < NT:
+                m_evac(iz, 0)
+                m_evac(iz, 1)
+            if 0 <= i2 < NT:
+                m_interleave(i2, 0)
+                m_interleave(i2, 1)
+            if j + 1 < NT:
+                ax_quantize(j + 1)
+            if i1 < NT:
+                stage1_bank(i1, 0)
+            if 0 <= i2 < NT:
+                m_quantize(i2)
+            if i1 < NT:
+                stage1_bank(i1, 1)
+                stage1_bank(i1, 2)
+                stage1_bank(i1, 3)
+            if 0 <= j - 1 < NT:
+                stats(j - 1)
+            if 0 <= iz < NT:
+                z_transposes(iz, 2)
+                z_transposes(iz, 3)
+                m_evac(iz, 2)
+                m_evac(iz, 3)
+            sort_ax(j + 2)
+            if 0 <= j - 1 < NT:
+                z_half(j - 1, 0)
+            if j < len(W2_SPLIT):
+                for n_unit in range(W2_SPLIT[j]):
+                    if w_loaded < 32:
+                        w_load(w_loaded)
+                        w_loaded += 1
+                    w_transpose(w_next)
+                    if n_unit == 0 and 0 <= j - 1 < NT:
+                        z_half(j - 1, 1)
+                    if n_unit > 0:
+                        w_quantize(w_next - 1)
+                    w_next += 1
+                w_quantize(w_next - 1)
+                if j == 1:
+                    nc.sync.dma_start(out=fb[:], in_=ff1_b.partition_broadcast(P))
+            else:
+                if 0 <= i2 < NT:
+                    stage2_bank(i2, 0)
+                if 0 <= j - 1 < NT:
+                    z_half(j - 1, 1)
+                if 0 <= i2 < NT:
+                    stage2_bank(i2, 1)
+                    relu_store(i2, 0)
+                    stage2_bank(i2, 2)
+                    stage2_bank(i2, 3)
+                    carried.append(i2)
+        for i_old in carried:
+            relu_store(i_old, 1)

@@ -20,8 +20,8 @@ KP = 4
 NB = 4
 EPS = 1e-5
 LZ = 2
-L2 = 3
-W2_SPLIT = (6, 5, 5)
+L2 = 4
+W2_SPLIT = (0, 6, 5, 5)
 
 FLOPS = 2 * 2 * SEQ * T * D * D
 
@@ -32,8 +32,7 @@ def tile_temporalatt_pb_l_kernel(tc, ax_cat, features, wout_w, ln_g, ln_b, ff1_w
         keep = ctx.enter_context(tc.tile_pool(name="keep", bufs=1))
         work = ctx.enter_context(tc.tile_pool(name="work", bufs=2))
         small = ctx.enter_context(tc.tile_pool(name="small", bufs=4))
-        tp_pool = ctx.enter_context(tc.psum_pool(name="tpp", bufs=4))
-        mm_pool = ctx.enter_context(tc.psum_pool(name="mmp", bufs=4))
+        psum = ctx.enter_context(tc.psum_pool(name="psum", bufs=8))
 
         eps_t = keep.tile([P, 1], F32, name="eps_t", tag="eps_t")
         nc.vector.memset(eps_t[:], EPS)
@@ -67,7 +66,7 @@ def tile_temporalatt_pb_l_kernel(tc, ax_cat, features, wout_w, ln_g, ln_b, ff1_w
             return grp
 
         def word_transposes(words_of, h):
-            bank = tp_pool.tile([P, 512], F32, name="tpb", tag="tpb")
+            bank = psum.tile([P, 512], F32, name="bank", tag="bank")
             for g2 in range(2):
                 for u in range(2):
                     c0 = (2 * g2 + u) * P
@@ -100,7 +99,7 @@ def tile_temporalatt_pb_l_kernel(tc, ax_cat, features, wout_w, ln_g, ln_b, ff1_w
             grp = new_grp()
             for h in range(2):
                 bank = word_transposes(lambda g, u: raw_w[:, 256 * g + u:256 * (g + 1):2], h)
-                word_evac(h == 0, grp, bank, h)
+                word_evac(h == 0 or n % 2 == 1, grp, bank, h)
             w_grp[n] = grp
 
         def w_quantize(n):
@@ -149,11 +148,16 @@ def tile_temporalatt_pb_l_kernel(tc, ax_cat, features, wout_w, ln_g, ln_b, ff1_w
                 srts[i] = srt
 
         def ax_transposes(i):
-            srt_w = srts.pop(i)[:].bitcast(F32)
             axg[i] = new_grp()
             axb[i] = []
-            for h in range(2):
-                axb[i].append(word_transposes(lambda g, u: srt_w[:, (2 * g + u) * P:(2 * g + u + 1) * P], h))
+            if i in srts:
+                srt_w = srts.pop(i)[:].bitcast(F32)
+                for h in range(2):
+                    axb[i].append(word_transposes(lambda g, u: srt_w[:, (2 * g + u) * P:(2 * g + u + 1) * P], h))
+            else:
+                raw_w = raws.pop(i)[:].bitcast(F32)
+                for h in range(2):
+                    axb[i].append(word_transposes(lambda g, u: raw_w[:, 256 * g + u:256 * (g + 1):2], h))
 
         def ax_evac(i, h):
             word_evac(h == 0, axg[i], axb[i][h], h)
@@ -167,7 +171,7 @@ def tile_temporalatt_pb_l_kernel(tc, ax_cat, features, wout_w, ln_g, ln_b, ff1_w
             axqs[i] = (q, sc)
 
         def mx_group(q, sc, wq, ws, b):
-            ps = mm_pool.tile([P, 512], F32, name="mmb", tag="mmb")
+            ps = psum.tile([P, 512], F32, name="bank", tag="bank")
             for kp in range(KP):
                 nc.tensor.matmul_mx(out=ps[:],
                                     lhsT=q[:, kp * P:(kp + 1) * P].bitcast(FP8X4),
@@ -227,7 +231,7 @@ def tile_temporalatt_pb_l_kernel(tc, ax_cat, features, wout_w, ln_g, ln_b, ff1_w
 
         def z_transposes(i, g):
             z = zs[i]
-            bank = tp_pool.tile([P, 512], F32, name="tpb", tag="tpb")
+            bank = psum.tile([P, 512], F32, name="bank", tag="bank")
             for t in range(4):
                 nc.tensor.transpose(bank[:, t * P:(t + 1) * P],
                                     z[:, 512 * t + P * g:512 * t + P * (g + 1)], ident[:])
@@ -256,8 +260,8 @@ def tile_temporalatt_pb_l_kernel(tc, ax_cat, features, wout_w, ln_g, ln_b, ff1_w
 
         def m_quantize(i):
             grp = mgrp.pop(i)
-            q = work.tile([P, KP * P], U32, name="mq", tag="mq", bufs=2, align_bytes=64)
-            sc = work.tile([P, KP * P], U8, name="ms", tag="ms", bufs=2, align_bytes=64)
+            q = work.tile([P, KP * P], U32, name="mq", tag="mq", bufs=3, align_bytes=64)
+            sc = work.tile([P, KP * P], U8, name="ms", tag="ms", bufs=3, align_bytes=64)
             nc.vector.quantize_mx(out=q[:].bitcast(FP8X4), scales=sc[:], in_=grp[:])
             mqs[i] = (q, sc)
 
@@ -272,118 +276,129 @@ def tile_temporalatt_pb_l_kernel(tc, ax_cat, features, wout_w, ln_g, ln_b, ff1_w
             if b == NB - 1:
                 mqs.pop(i)
 
-        def relu_store(i, h):
+        def relu_store(i, lo, hi):
             s, t0 = tok(i)
             o = os_d[i]
-            lo, hi = 1024 * h, 1024 * (h + 1)
             nc.scalar.activation(out=o[:, lo:hi], in_=o[:, lo:hi], func=ACT.Relu)
-            nc.scalar.dma_start(out=out[s, t0:t0 + P, lo:hi], in_=o[:, lo:hi])
-            if h == 1:
+            nc.sync.dma_start(out=out[s, t0:t0 + P, lo:hi], in_=o[:, lo:hi])
+            if hi == D:
                 os_d.pop(i)
 
+        w_load(0)
+        w_load(1)
         load_ax(0)
+        w_load(2)
+        w_load(3)
         nc.sync.dma_start(out=g_raw[:].rearrange("p (g t) -> p g t", g=4, t=4),
                           in_=ln_g.rearrange("(g p t) -> p g t", g=4, p=P, t=4))
         nc.sync.dma_start(out=b_raw[:].rearrange("p (g t) -> p g t", g=4, t=4),
                           in_=ln_b.rearrange("(g p t) -> p g t", g=4, p=P, t=4))
-        w_load(0)
-        w_load(1)
-        w_load(2)
+        load_x(0)
+        for n in range(16):
+            w_transpose(n)
+            w_load(n + 4)
+            if n == 1:
+                ax_transposes(0)
+                ax_evac(0, 0)
+                ax_evac(0, 1)
+            if n == 4:
+                load_ax(1)
+            if n == 8:
+                sort_ax(1)
+            if n == 9:
+                ax_transposes(1)
+                ax_evac(1, 0)
+                ax_evac(1, 1)
+            if n > 0:
+                w_quantize(n - 1)
+            if n == 2:
+                ax_quantize(0)
+            if n == 10:
+                ax_quantize(1)
+            if n == 11:
+                load_ax(2)
+                load_x(1)
+            if n == 14:
+                sort_ax(2)
+            if n > 3 and n % 4 == 0:
+                stage1_bank(0, n // 4 - 1)
+        load_ax(3)
+        load_x(2)
+        w_quantize(15)
         nc.vector.tensor_copy(out=g_col[:], in_=g_raw[:])
         nc.vector.tensor_copy(out=b_col[:], in_=b_raw[:])
-        sort_ax(0)
-        ax_transposes(0)
-        ax_evac(0, 0)
-        ax_evac(0, 1)
-        for n in range(16):
-            if n + 3 < 16:
-                w_load(n + 3)
-            if n == 8:
-                load_x(0)
-            if n == 10:
-                load_ax(1)
-            if n == 12:
-                load_x(1)
-            if n == 13:
-                load_ax(2)
-            w_transpose(n)
-            if n == 0:
-                ax_quantize(0)
-            else:
-                w_quantize(n - 1)
-        w_load(16)
-        w_load(17)
-        sort_ax(1)
-        w_quantize(15)
         w_next = 16
-        w_loaded = 18
+        w_loaded = 20
 
         carried = []
-        for j in range(NT + L2):
+        for j in range(1, NT + L2):
             i1, iz, i2 = j, j - LZ, j - L2
-            load_ax(j + 3)
-            load_x(j + 2)
+            has1 = i1 < NT
+            hasz = 0 <= iz < NT
+            has2 = 0 <= i2 < NT
+            hasn = j - 1 < NT
             if j + 1 < NT:
                 ax_transposes(j + 1)
-            if 0 <= iz < NT:
-                z_transposes(iz, 0)
-                z_transposes(iz, 1)
+            if hasz:
+                for g in range(KP):
+                    z_transposes(iz, g)
+            if j == 1:
+                stage1_bank(0, 3)
+                stats(0)
+            load_ax(j + 3)
+            load_x(j + 2)
             if j + 1 < NT:
                 ax_evac(j + 1, 0)
                 ax_evac(j + 1, 1)
             for i_old in carried:
-                relu_store(i_old, 1)
+                relu_store(i_old, 1024, D)
             carried = []
-            if 0 <= iz < NT:
-                m_evac(iz, 0)
-                m_evac(iz, 1)
-            if 0 <= i2 < NT:
-                m_interleave(i2, 0)
-                m_interleave(i2, 1)
+            if hasz:
+                for g in range(KP):
+                    m_evac(iz, g)
             if j + 1 < NT:
                 ax_quantize(j + 1)
-            if i1 < NT:
-                stage1_bank(i1, 0)
-            if 0 <= i2 < NT:
-                m_quantize(i2)
-            if i1 < NT:
-                stage1_bank(i1, 1)
-                stage1_bank(i1, 2)
-                stage1_bank(i1, 3)
-            if 0 <= j - 1 < NT:
-                stats(j - 1)
-            if 0 <= iz < NT:
-                z_transposes(iz, 2)
-                z_transposes(iz, 3)
-                m_evac(iz, 2)
-                m_evac(iz, 3)
-            sort_ax(j + 2)
-            if 0 <= j - 1 < NT:
+            if hasn:
                 z_half(j - 1, 0)
+                z_half(j - 1, 1)
+            if has1:
+                stage1_bank(i1, 0)
+            if hasz:
+                m_interleave(iz, 0)
+            if has1:
+                stage1_bank(i1, 1)
+            if hasz:
+                m_interleave(iz, 1)
+            if has1:
+                stage1_bank(i1, 2)
+            if hasz:
+                m_quantize(iz)
+            if has1:
+                stage1_bank(i1, 3)
+            sort_ax(j + 2)
+            if has1:
+                stats(i1)
             if j < len(W2_SPLIT):
                 for n_unit in range(W2_SPLIT[j]):
+                    w_transpose(w_next)
                     if w_loaded < 32:
                         w_load(w_loaded)
                         w_loaded += 1
-                    w_transpose(w_next)
-                    if n_unit == 0 and 0 <= j - 1 < NT:
-                        z_half(j - 1, 1)
                     if n_unit > 0:
                         w_quantize(w_next - 1)
                     w_next += 1
                 w_quantize(w_next - 1)
-                if j == 1:
+                if j == 2:
                     nc.sync.dma_start(out=fb[:], in_=ff1_b.partition_broadcast(P))
-            else:
-                if 0 <= i2 < NT:
+            elif has2:
+                if i2 < NT - 1:
                     stage2_bank(i2, 0)
-                if 0 <= j - 1 < NT:
-                    z_half(j - 1, 1)
-                if 0 <= i2 < NT:
                     stage2_bank(i2, 1)
-                    relu_store(i2, 0)
+                    relu_store(i2, 0, 1024)
                     stage2_bank(i2, 2)
                     stage2_bank(i2, 3)
                     carried.append(i2)
-        for i_old in carried:
-            relu_store(i_old, 1)
+                else:
+                    for b in range(NB):
+                        stage2_bank(i2, b)
+                        relu_store(i2, 512 * b, 512 * (b + 1))

@@ -18,8 +18,10 @@ T = 2048
 NT = SEQ * T // P
 KP = 4
 NB = 4
+H = D // 2
+VR = 1536
 EPS = 1e-5
-LZ = 2
+LZ = 3
 L2 = 4
 W2_SPLIT = (0, 6, 5, 5)
 
@@ -48,6 +50,8 @@ def tile_temporalatt_pb_l_kernel(tc, ax_cat, features, wout_w, ln_g, ln_b, ff1_w
         w2q = keep.tile([P, KP, D], U32, name="w2q", tag="w2q", align_bytes=64)
         w2s = keep.tile([P, KP, D], U8, name="w2s", tag="w2s", align_bytes=64)
         fb = keep.tile([P, D], BF16, name="fb", tag="fb")
+        gs = keep.tile([P, H], BF16, name="gs", tag="gs")
+        bs = keep.tile([P, H], BF16, name="bs", tag="bs")
         g_raw = keep.tile([P, 16], BF16, name="g_raw", tag="g_raw")
         b_raw = keep.tile([P, 16], BF16, name="b_raw", tag="b_raw")
         g_col = keep.tile([P, 16], F32, name="g_col", tag="g_col")
@@ -56,10 +60,10 @@ def tile_temporalatt_pb_l_kernel(tc, ax_cat, features, wout_w, ln_g, ln_b, ff1_w
         def tok(i):
             return i // (T // P), (i % (T // P)) * P
 
-        def load_rows(rows):
-            raw = work.tile([P, D], BF16, name="raw", tag="raw", bufs=4)
-            nc.sync.dma_start(out=raw[:], in_=rows)
-            return raw
+        def load_rows_h(rows):
+            nat = work.tile([P, H], BF16, name="nat", tag="nat", bufs=2)
+            nc.sync.dma_start(out=nat[:], in_=rows)
+            return nat
 
         def new_grp():
             grp = work.tile([P, D], BF16, name="grp", tag="grp", bufs=3, align_bytes=64)
@@ -82,33 +86,83 @@ def tile_temporalatt_pb_l_kernel(tc, ax_cat, features, wout_w, ln_g, ln_b, ff1_w
                 nc.vector.tensor_copy(out=dst, in_=src)
 
         w1_rows = wout_w.rearrange("(g p t) k -> g t p k", g=4, p=P, t=4)
-        w_units = []
-        for t in range(4):
-            for g in range(4):
-                w_units.append((w1_rows[g, t], w1q, w1s, 512 * t + P * g))
+        w_rows = []
+        for u in range(2):
+            for g in range(2):
+                for e in range(2):
+                    w_rows.append(w1_rows[g, 2 * u + e])
+        w_cols = {}
+        for tp in range(2):
+            for t2 in range(2):
+                for g2 in range(2):
+                    w_cols[len(w_rows)] = (w1q, w1s, H + 256 * (2 * tp + t2) + P * g2)
+                    w_rows.append(w1_rows[2 + g2, 2 * tp + t2])
         for rt in range(16):
-            w_units.append((ff1_w[rt * P:(rt + 1) * P, :], w2q, w2s, rt * P))
+            w_cols[len(w_rows)] = (w2q, w2s, rt * P)
+            w_rows.append(ff1_w[rt * P:(rt + 1) * P, :])
+        NPAIR = 8
         w_raw = {}
         w_grp = {}
 
-        def w_load(n):
-            w_raw[n] = load_rows(w_units[n][0])
+        w_count = [0]
+
+        def w_load(depth=7):
+            for unused in range(depth):
+                n = w_count[0]
+                if len(w_raw) < depth and n < len(w_rows):
+                    if n % 7 < 4:
+                        raw = work.tile([P, D], BF16, name="raw", tag="raw", bufs=4)
+                    else:
+                        raw = work.tile([P, D], BF16, name="o", tag="o", bufs=3)
+                    nc.sync.dma_start(out=raw[:], in_=w_rows[n])
+                    w_raw[n] = raw
+                    w_count[0] += 1
 
         def w_transpose(n):
-            raw_w = w_raw.pop(n)[:].bitcast(F32)
             grp = new_grp()
-            for h in range(2):
-                bank = word_transposes(lambda g, u: raw_w[:, 256 * g + u:256 * (g + 1):2], h)
-                word_evac(h == 0 or n % 2 == 1, grp, bank, h)
+            if n < NPAIR:
+                h = n % 2
+                pair = (w_raw[n - h][:].bitcast(F32), w_raw[n - h + 1][:].bitcast(F32))
+                for k2 in range(2):
+                    kp = 2 * h + k2
+                    bank = psum.tile([P, 512], F32, name="bank", tag="bank")
+                    for e in range(2):
+                        for u in range(2):
+                            c0 = (2 * e + u) * P
+                            nc.tensor.transpose(bank[:, c0:c0 + P], pair[e][:, 256 * kp + u:256 * (kp + 1):2],
+                                                ident[:])
+                    dst = grp[:].bitcast(F32).rearrange("p (k w e u) -> p k w e u", k=2, w=P, e=2, u=2)[:, k2]
+                    src = bank[:].rearrange("p (e u w) -> p w e u", e=2, u=2, w=P)
+                    if k2 == 0 or n % 2 == 1:
+                        nc.scalar.copy(out=dst, in_=src)
+                    else:
+                        nc.vector.tensor_copy(out=dst, in_=src)
+                if h == 1:
+                    w_raw.pop(n - 1)
+                    w_raw.pop(n)
+            else:
+                raw_w = w_raw.pop(n)[:].bitcast(F32)
+                for h in range(2):
+                    bank = word_transposes(lambda g, u: raw_w[:, 256 * g + u:256 * (g + 1):2], h)
+                    word_evac(h == 0 or n % 2 == 1, grp, bank, h)
             w_grp[n] = grp
 
         def w_quantize(n):
             grp = w_grp.pop(n)
-            wq, ws, col0 = w_units[n][1], w_units[n][2], w_units[n][3]
-            for kp in range(KP):
-                nc.vector.quantize_mx(out=wq[:, kp, col0:col0 + P].bitcast(FP8X4),
-                                      scales=ws[:, kp, col0:col0 + P],
-                                      in_=grp[:, 512 * kp:512 * (kp + 1)])
+            if n < NPAIR:
+                q4 = n // 2
+                col0 = 512 * (q4 // 2) + 256 * (q4 % 2)
+                for k2 in range(2):
+                    kp = 2 * (n % 2) + k2
+                    nc.vector.quantize_mx(out=w1q[:, kp, col0:col0 + 256].bitcast(FP8X4),
+                                          scales=w1s[:, kp, col0:col0 + 256],
+                                          in_=grp[:, 1024 * k2:1024 * (k2 + 1)])
+            else:
+                wq, ws, col0 = w_cols[n]
+                for kp in range(KP):
+                    nc.vector.quantize_mx(out=wq[:, kp, col0:col0 + P].bitcast(FP8X4),
+                                          scales=ws[:, kp, col0:col0 + P],
+                                          in_=grp[:, 512 * kp:512 * (kp + 1)])
 
         raws = {}
         srts = {}
@@ -160,7 +214,7 @@ def tile_temporalatt_pb_l_kernel(tc, ax_cat, features, wout_w, ln_g, ln_b, ff1_w
                     axb[i].append(word_transposes(lambda g, u: raw_w[:, 256 * g + u:256 * (g + 1):2], h))
 
         def ax_evac(i, h):
-            word_evac(h == 0, axg[i], axb[i][h], h)
+            word_evac(True, axg[i], axb[i][h], h)
 
         def ax_quantize(i):
             grp = axg.pop(i)
@@ -189,10 +243,18 @@ def tile_temporalatt_pb_l_kernel(tc, ax_cat, features, wout_w, ln_g, ln_b, ff1_w
                 sums_d[i] = sums_new
             q, sc = axqs[i]
             ps = mx_group(q, sc, w1q, w1s, t)
-            xv = xs[i][:].rearrange("p (v t) -> p t v", t=4)
-            nc.vector.scalar_tensor_tensor(out=rs[i][:, 512 * t:512 * (t + 1)], in0=ps[:], scalar=0.0,
-                                           in1=xv[:, t, :], op0=ALU.add, op1=ALU.add,
-                                           accum_out=sums_d[i][:, t:t + 1])
+            r_b = rs[i][:, 512 * t:512 * (t + 1)]
+            if t < 2:
+                nc.vector.scalar_tensor_tensor(out=r_b.rearrange("p (v e) -> p v e", e=2),
+                                               in0=ps[:].rearrange("p (v e) -> p v e", e=2), scalar=0.0,
+                                               in1=xs[i][:, 0:H].rearrange("p (v u e) -> p u v e", u=2, e=2)[:, t],
+                                               op0=ALU.add, op1=ALU.add, accum_out=sums_d[i][:, t:t + 1])
+            else:
+                c_lo = 2 * (t - 2)
+                nc.vector.scalar_tensor_tensor(out=r_b.rearrange("p (c v) -> p c v", c=2),
+                                               in0=ps[:].rearrange("p (c v) -> p c v", c=2), scalar=0.0,
+                                               in1=xs[i][:, H:D].rearrange("p (v c) -> p c v", c=4)[:, c_lo:c_lo + 2],
+                                               op0=ALU.add, op1=ALU.add, accum_out=sums_d[i][:, t:t + 1])
             if t == NB - 1:
                 axqs.pop(i)
                 xs.pop(i)
@@ -211,52 +273,70 @@ def tile_temporalatt_pb_l_kernel(tc, ax_cat, features, wout_w, ln_g, ln_b, ff1_w
             nc.scalar.activation(out=std[:], in_=ssq[:], func=ACT.Sqrt, bias=eps_t[:], scale=1.0 / D)
             stat[i] = (negmu, std)
 
-        def z_half(i, h):
-            if h == 0:
-                negmu, std = stat[i]
-                rstd = small.tile([P, 1], F32, name="rstd", tag="rstd")
-                nc.vector.reciprocal(out=rstd[:], in_=std[:])
-                z_new = work.tile([P, D], F32, name="z", tag="z", bufs=2)
-                zs[i] = z_new
-                stat[i] = (negmu, rstd)
+        us = {}
+        m1s = {}
+
+        def apply_start(i):
+            negmu, std = stat[i]
+            rstd = small.tile([P, 1], F32, name="rstd", tag="rstd")
+            nc.vector.reciprocal(out=rstd[:], in_=std[:])
+            stat[i] = (negmu, rstd)
+
+        def apply_z(i):
             negmu, rstd = stat[i]
-            lo, hi = 1024 * h, 1024 * (h + 1)
-            nc.vector.tensor_scalar(out=zs[i][:, lo:hi], in0=rs[i][:, lo:hi], scalar1=negmu[:], scalar2=rstd[:],
+            z_new = work.tile([P, H], F32, name="z", tag="z", bufs=2)
+            zs[i] = z_new
+            nc.vector.tensor_scalar(out=z_new[:], in0=rs[i][:, H:D], scalar1=negmu[:], scalar2=rstd[:],
                                     op0=ALU.add, op1=ALU.mult)
+
+        def apply_u(i):
+            negmu, rstd = stat[i]
+            u_new = work.tile([P, H], F32, name="u", tag="u", bufs=1)
+            us[i] = u_new
+            nc.vector.scalar_tensor_tensor(out=u_new[:], in0=rs[i][:, 0:H], scalar=negmu[:], in1=gs[:],
+                                           op0=ALU.add, op1=ALU.mult)
+            rs.pop(i)
+
+        def apply_m(i, h):
+            negmu, rstd = stat[i]
+            if h == 0:
+                m1_new = work.tile([P, H], BF16, name="m1", tag="m1", bufs=2)
+                m1s[i] = m1_new
+            lo, hi = 512 * h, 512 * (h + 1)
+            nc.vector.scalar_tensor_tensor(out=m1s[i][:, lo:hi], in0=us[i][:, lo:hi], scalar=rstd[:],
+                                           in1=bs[:, lo:hi], op0=ALU.mult, op1=ALU.add)
             if h == 1:
+                us.pop(i)
                 stat.pop(i)
-                rs.pop(i)
 
         zb = {}
 
-        def z_transposes(i, g):
-            z = zs[i]
-            bank = psum.tile([P, 512], F32, name="bank", tag="bank")
-            for t in range(4):
-                nc.tensor.transpose(bank[:, t * P:(t + 1) * P],
-                                    z[:, 512 * t + P * g:512 * t + P * (g + 1)], ident[:])
-            zb[(i, g)] = bank
-            if g == KP - 1:
-                zs.pop(i)
+        def m_transposes(i):
+            m1_w = m1s.pop(i)[:].bitcast(F32)
+            zb[(i, 0)] = word_transposes(lambda g, u: m1_w[:, 256 * u + P * g:256 * u + P * (g + 1)], 0)
+            z = zs.pop(i)
+            for g2 in range(2):
+                bank = psum.tile([P, 512], F32, name="bank", tag="bank")
+                for t in range(4):
+                    nc.tensor.transpose(bank[:, t * P:(t + 1) * P],
+                                        z[:, 256 * t + P * g2:256 * t + P * (g2 + 1)], ident[:])
+                zb[(i, 1 + g2)] = bank
 
-        def m_evac(i, g):
-            if g == 0:
-                mt_new = work.tile([P, D], BF16, name="mt", tag="mt", bufs=2)
-                mts[i] = mt_new
-            bank = zb.pop((i, g))
-            for t in range(4):
-                c = 4 * g + t
-                nc.scalar.activation(out=mts[i][:, c * P:(c + 1) * P], in_=bank[:, t * P:(t + 1) * P],
-                                     func=ACT.Identity, scale=g_col[:, c:c + 1], bias=b_col[:, c:c + 1])
+        def m_evac(i):
+            mgrp[i] = new_grp()
+            word_evac(True, mgrp[i], zb.pop((i, 0)), 0)
+            mt_new = work.tile([P, H], BF16, name="mt", tag="mt", bufs=2)
+            mts[i] = mt_new
+            for g2 in range(2):
+                bank = zb.pop((i, 1 + g2))
+                for t in range(4):
+                    c = 4 * g2 + t
+                    nc.scalar.activation(out=mt_new[:, c * P:(c + 1) * P], in_=bank[:, t * P:(t + 1) * P],
+                                         func=ACT.Identity, scale=g_col[:, 8 + c:9 + c], bias=b_col[:, 8 + c:9 + c])
 
-        def m_interleave(i, h):
-            if h == 0:
-                mgrp[i] = new_grp()
-            lo, hi = 1024 * h, 1024 * (h + 1)
-            nc.vector.tensor_copy(out=mgrp[i][:, lo:hi].rearrange("p (g c t) -> p g c t", g=2, c=P, t=4),
-                                  in_=mts[i][:, lo:hi].rearrange("p (g t c) -> p g c t", g=2, t=4, c=P))
-            if h == 1:
-                mts.pop(i)
+        def m_interleave(i):
+            nc.vector.tensor_copy(out=mgrp[i][:, H:D].rearrange("p (g c t) -> p g c t", g=2, c=P, t=4),
+                                  in_=mts.pop(i)[:].rearrange("p (g t c) -> p g c t", g=2, t=4, c=P))
 
         def m_quantize(i):
             grp = mgrp.pop(i)
@@ -265,14 +345,22 @@ def tile_temporalatt_pb_l_kernel(tc, ax_cat, features, wout_w, ln_g, ln_b, ff1_w
             nc.vector.quantize_mx(out=q[:].bitcast(FP8X4), scales=sc[:], in_=grp[:])
             mqs[i] = (q, sc)
 
+        ovs = {}
+
         def stage2_bank(i, b):
             if b == 0:
                 o_new = work.tile([P, D], F32, name="o", tag="o", bufs=3)
                 os_d[i] = o_new
             q, sc = mqs[i]
             ps = mx_group(q, sc, w2q, w2s, b)
-            nc.vector.tensor_tensor(out=os_d[i][:, 512 * b:512 * (b + 1)], in0=ps[:],
-                                    in1=fb[:, 512 * b:512 * (b + 1)], op=ALU.add)
+            if 512 * b >= VR and i < NT - 1:
+                if 512 * b == VR:
+                    ov_new = work.tile([P, D - VR], F32, name="ov", tag="ov", bufs=2)
+                    ovs[i] = ov_new
+                dst = ovs[i][:, 512 * b - VR:512 * (b + 1) - VR]
+            else:
+                dst = os_d[i][:, 512 * b:512 * (b + 1)]
+            nc.vector.tensor_tensor(out=dst, in0=ps[:], in1=fb[:, 512 * b:512 * (b + 1)], op=ALU.add)
             if b == NB - 1:
                 mqs.pop(i)
 
@@ -284,24 +372,26 @@ def tile_temporalatt_pb_l_kernel(tc, ax_cat, features, wout_w, ln_g, ln_b, ff1_w
             if hi == D:
                 os_d.pop(i)
 
-        w_load(0)
-        w_load(1)
-        load_ax(0)
+        def relu_store_shared(i):
+            s, t0 = tok(i)
+            o = os_d.pop(i)
+            nc.vector.tensor_scalar_max(out=o[:, VR:D], in0=ovs.pop(i)[:], scalar1=0.0)
+            nc.scalar.activation(out=o[:, 0:VR], in_=o[:, 0:VR], func=ACT.Relu)
+            nc.sync.dma_start(out=out[s, t0:t0 + P, :], in_=o[:])
+
         w_load(2)
-        w_load(3)
-        nc.sync.dma_start(out=g_raw[:].rearrange("p (g t) -> p g t", g=4, t=4),
-                          in_=ln_g.rearrange("(g p t) -> p g t", g=4, p=P, t=4))
-        nc.sync.dma_start(out=b_raw[:].rearrange("p (g t) -> p g t", g=4, t=4),
-                          in_=ln_b.rearrange("(g p t) -> p g t", g=4, p=P, t=4))
-        load_x(0)
+        load_ax(0)
+        w_load()
         for n in range(16):
             w_transpose(n)
-            w_load(n + 4)
+            w_load()
             if n == 1:
                 ax_transposes(0)
                 ax_evac(0, 0)
                 ax_evac(0, 1)
-            if n == 4:
+            if n == 2:
+                load_x(0)
+            if n == 5:
                 load_ax(1)
             if n == 8:
                 sort_ax(1)
@@ -316,6 +406,8 @@ def tile_temporalatt_pb_l_kernel(tc, ax_cat, features, wout_w, ln_g, ln_b, ff1_w
             if n == 10:
                 ax_quantize(1)
             if n == 11:
+                g_nat = load_rows_h(ln_g[0:H].partition_broadcast(P))
+                b_nat = load_rows_h(ln_b[0:H].partition_broadcast(P))
                 load_ax(2)
                 load_x(1)
             if n == 14:
@@ -324,13 +416,19 @@ def tile_temporalatt_pb_l_kernel(tc, ax_cat, features, wout_w, ln_g, ln_b, ff1_w
                 stage1_bank(0, n // 4 - 1)
         load_ax(3)
         load_x(2)
+        nc.sync.dma_start(out=g_raw[:].rearrange("p (g t) -> p g t", g=4, t=4),
+                          in_=ln_g.rearrange("(g p t) -> p g t", g=4, p=P, t=4))
+        nc.sync.dma_start(out=b_raw[:].rearrange("p (g t) -> p g t", g=4, t=4),
+                          in_=ln_b.rearrange("(g p t) -> p g t", g=4, p=P, t=4))
         w_quantize(15)
-        nc.vector.tensor_copy(out=g_col[:], in_=g_raw[:])
-        nc.vector.tensor_copy(out=b_col[:], in_=b_raw[:])
+        nc.vector.tensor_copy(out=gs[:].rearrange("p (u v e) -> p u v e", u=2, e=2),
+                              in_=g_nat[:].rearrange("p (v u e) -> p u v e", u=2, e=2))
+        nc.vector.tensor_copy(out=bs[:].rearrange("p (u v e) -> p u v e", u=2, e=2),
+                              in_=b_nat[:].rearrange("p (v u e) -> p u v e", u=2, e=2))
         w_next = 16
-        w_loaded = 20
 
         carried = []
+        quantized = {}
         for j in range(1, NT + L2):
             i1, iz, i2 = j, j - LZ, j - L2
             has1 = i1 < NT
@@ -340,50 +438,57 @@ def tile_temporalatt_pb_l_kernel(tc, ax_cat, features, wout_w, ln_g, ln_b, ff1_w
             if j + 1 < NT:
                 ax_transposes(j + 1)
             if hasz:
-                for g in range(KP):
-                    z_transposes(iz, g)
+                m_transposes(iz)
             if j == 1:
                 stage1_bank(0, 3)
-                stats(0)
             load_ax(j + 3)
             load_x(j + 2)
             if j + 1 < NT:
                 ax_evac(j + 1, 0)
                 ax_evac(j + 1, 1)
-            for i_old in carried:
-                relu_store(i_old, 1024, D)
-            carried = []
-            if hasz:
-                for g in range(KP):
-                    m_evac(iz, g)
-            if j + 1 < NT:
-                ax_quantize(j + 1)
+            late = j >= NT - 1
+            if late and hasz:
+                m_evac(iz)
             if hasn:
-                z_half(j - 1, 0)
-                z_half(j - 1, 1)
+                stats(j - 1)
+            for i_old in carried:
+                relu_store_shared(i_old)
+            carried = []
+            if hasz and not late:
+                m_evac(iz)
+            sort_ax(j + 2)
+            if 0 <= iz - 1 < NT and (iz - 1) not in quantized:
+                m_interleave(iz - 1)
             if has1:
                 stage1_bank(i1, 0)
-            if hasz:
-                m_interleave(iz, 0)
+            if 0 <= iz - 1 < NT and (iz - 1) not in quantized:
+                m_quantize(iz - 1)
             if has1:
                 stage1_bank(i1, 1)
-            if hasz:
-                m_interleave(iz, 1)
+            if j + 1 < NT:
+                ax_quantize(j + 1)
             if has1:
                 stage1_bank(i1, 2)
-            if hasz:
-                m_quantize(iz)
+            if late and has1:
+                m_interleave(iz)
             if has1:
                 stage1_bank(i1, 3)
-            sort_ax(j + 2)
-            if has1:
-                stats(i1)
+            if late and has1:
+                m_quantize(iz)
+                quantized[iz] = True
+            if hasn and has1:
+                apply_start(j - 1)
+                apply_z(j - 1)
+                apply_u(j - 1)
+            if j == 1:
+                nc.vector.tensor_copy(out=g_col[:], in_=g_raw[:])
+                nc.vector.tensor_copy(out=b_col[:], in_=b_raw[:])
             if j < len(W2_SPLIT):
                 for n_unit in range(W2_SPLIT[j]):
                     w_transpose(w_next)
-                    if w_loaded < 32:
-                        w_load(w_loaded)
-                        w_loaded += 1
+                    w_load()
+                    if n_unit < 2:
+                        apply_m(j - 1, n_unit)
                     if n_unit > 0:
                         w_quantize(w_next - 1)
                     w_next += 1
@@ -393,10 +498,24 @@ def tile_temporalatt_pb_l_kernel(tc, ax_cat, features, wout_w, ln_g, ln_b, ff1_w
             elif has2:
                 if i2 < NT - 1:
                     stage2_bank(i2, 0)
+                    if hasn and has1:
+                        apply_m(j - 1, 0)
                     stage2_bank(i2, 1)
-                    relu_store(i2, 0, 1024)
+                    if hasn and has1:
+                        apply_m(j - 1, 1)
+                    if hasz and not has1:
+                        m_interleave(iz)
                     stage2_bank(i2, 2)
+                    if hasz and not has1:
+                        m_quantize(iz)
+                        quantized[iz] = True
                     stage2_bank(i2, 3)
+                    if hasn and not has1:
+                        apply_start(j - 1)
+                        apply_z(j - 1)
+                        apply_u(j - 1)
+                        apply_m(j - 1, 0)
+                        apply_m(j - 1, 1)
                     carried.append(i2)
                 else:
                     for b in range(NB):

@@ -44,6 +44,10 @@ def tile_temporalatt_pb_l_kernel(tc, ax_cat, features, wout_w, ln_g, ln_b, ff1_w
         ident = keep.tile([P, P], F32, name="ident", tag="ident")
         make_identity(nc, ident[:])
         ctx.enter_context(tc.manual_schedule())
+        ones = keep.tile([P, P], BF16, name="ones", tag="ones")
+        nc.vector.memset(ones[:], 1.0)
+        rowt = keep.tile([P, D], BF16, name="rowt", tag="rowt")
+        nc.vector.memset(rowt[:], 0.0)
 
         w1q = keep.tile([P, KP, D], U32, name="w1q", tag="w1q", align_bytes=64)
         w1s = keep.tile([P, KP, D], U8, name="w1s", tag="w1s", align_bytes=64)
@@ -59,11 +63,6 @@ def tile_temporalatt_pb_l_kernel(tc, ax_cat, features, wout_w, ln_g, ln_b, ff1_w
 
         def tok(i):
             return i // (T // P), (i % (T // P)) * P
-
-        def load_rows_h(rows):
-            nat = work.tile([P, H], BF16, name="nat", tag="nat", bufs=2)
-            nc.sync.dma_start(out=nat[:], in_=rows)
-            return nat
 
         def new_grp():
             grp = work.tile([P, D], BF16, name="grp", tag="grp", bufs=3, align_bytes=64)
@@ -114,9 +113,14 @@ def tile_temporalatt_pb_l_kernel(tc, ax_cat, features, wout_w, ln_g, ln_b, ff1_w
                         raw = work.tile([P, D], BF16, name="raw", tag="raw", bufs=4)
                     else:
                         raw = work.tile([P, D], BF16, name="o", tag="o", bufs=3)
-                    nc.sync.dma_start(out=raw[:], in_=w_rows[n])
+                    if n > 1:
+                        nc.sync.dma_start(out=raw[:], in_=w_rows[n])
                     w_raw[n] = raw
                     w_count[0] += 1
+                    if n == 1:
+                        for k_lo in (0, H):
+                            for n01 in range(2):
+                                nc.sync.dma_start(out=w_raw[n01][:, k_lo:k_lo + H], in_=w_rows[n01][:, k_lo:k_lo + H])
 
         def w_transpose(n):
             grp = new_grp()
@@ -380,6 +384,8 @@ def tile_temporalatt_pb_l_kernel(tc, ax_cat, features, wout_w, ln_g, ln_b, ff1_w
             nc.sync.dma_start(out=out[s, t0:t0 + P, :], in_=o[:])
 
         w_load(2)
+        nc.sync.dma_start(out=rowt[0:1, 0:H], in_=ln_g[0:H].rearrange("(o c) -> o c", o=1))
+        nc.sync.dma_start(out=rowt[0:1, H:D], in_=ln_b[0:H].rearrange("(o c) -> o c", o=1))
         load_ax(0)
         w_load()
         for n in range(16):
@@ -389,6 +395,14 @@ def tile_temporalatt_pb_l_kernel(tc, ax_cat, features, wout_w, ln_g, ln_b, ff1_w
                 ax_transposes(0)
                 ax_evac(0, 0)
                 ax_evac(0, 1)
+            if n == 3:
+                for k in range(4):
+                    bank = psum.tile([P, 512], F32, name="bank", tag="bank")
+                    nc.tensor.matmul(out=bank[:], lhsT=ones[:], rhs=rowt[:, 512 * k:512 * (k + 1)], start=True, stop=True)
+                    spread = (gs, bs)[k // 2]
+                    v_lo = P * (k % 2)
+                    nc.scalar.copy(out=spread[:].rearrange("p (u v e) -> p u v e", u=2, e=2)[:, :, v_lo:v_lo + P, :],
+                                   in_=bank[:].rearrange("p (v u e) -> p u v e", u=2, e=2))
             if n == 2:
                 load_x(0)
             if n == 5:
@@ -406,8 +420,6 @@ def tile_temporalatt_pb_l_kernel(tc, ax_cat, features, wout_w, ln_g, ln_b, ff1_w
             if n == 10:
                 ax_quantize(1)
             if n == 11:
-                g_nat = load_rows_h(ln_g[0:H].partition_broadcast(P))
-                b_nat = load_rows_h(ln_b[0:H].partition_broadcast(P))
                 load_ax(2)
                 load_x(1)
             if n == 14:
@@ -421,10 +433,6 @@ def tile_temporalatt_pb_l_kernel(tc, ax_cat, features, wout_w, ln_g, ln_b, ff1_w
         nc.sync.dma_start(out=b_raw[:].rearrange("p (g t) -> p g t", g=4, t=4),
                           in_=ln_b.rearrange("(g p t) -> p g t", g=4, p=P, t=4))
         w_quantize(15)
-        nc.vector.tensor_copy(out=gs[:].rearrange("p (u v e) -> p u v e", u=2, e=2),
-                              in_=g_nat[:].rearrange("p (v u e) -> p u v e", u=2, e=2))
-        nc.vector.tensor_copy(out=bs[:].rearrange("p (u v e) -> p u v e", u=2, e=2),
-                              in_=b_nat[:].rearrange("p (v u e) -> p u v e", u=2, e=2))
         w_next = 16
 
         carried = []

from contextlib import ExitStack

import concourse.mybir as mybir
from concourse.masks import make_identity

F32 = mybir.dt.float32
BF16 = mybir.dt.bfloat16
U32 = mybir.dt.uint32
U8 = mybir.dt.uint8
FP8X4 = mybir.dt.float8_e4m3fn_x4
ALU = mybir.AluOpType
ACT = mybir.ActivationFunctionType

P = 128
D = 2048
SEQ = 2
T = 2048
NT = SEQ * T // P
KP = 4
NB = 4
H = D // 2
VR = 1536
EPS = 1e-5
LZ = 3
L2 = 4
W2_SPLIT = (0, 6, 5, 5)

FLOPS = 2 * 2 * SEQ * T * D * D


def tile_temporalatt_pb_l_kernel(tc, ax_cat, features, wout_w, ln_g, ln_b, ff1_w, ff1_b, out):
    nc = tc.nc
    with ExitStack() as ctx:
        keep = ctx.enter_context(tc.tile_pool(name="keep", bufs=1))
        work = ctx.enter_context(tc.tile_pool(name="work", bufs=2))
        small = ctx.enter_context(tc.tile_pool(name="small", bufs=4))
        psum = ctx.enter_context(tc.psum_pool(name="psum", bufs=8))

        eps_t = keep.tile([P, 1], F32, name="eps_t", tag="eps_t")
        nc.vector.memset(eps_t[:], EPS)
        warm = keep.tile([P, 1], F32, name="warm", tag="warm")
        nc.scalar.activation(out=warm[:], in_=eps_t[:], func=ACT.Sqrt)

        ident = keep.tile([P, P], F32, name="ident", tag="ident")
        make_identity(nc, ident[:])
        ctx.enter_context(tc.manual_schedule())
        ones = keep.tile([P, P], BF16, name="ones", tag="ones")
        nc.vector.memset(ones[:], 1.0)
        rowt = keep.tile([P, D], BF16, name="rowt", tag="rowt")
        nc.vector.memset(rowt[:], 0.0)

        w1q = keep.tile([P, KP, D], U32, name="w1q", tag="w1q", align_bytes=64)
        w1s = keep.tile([P, KP, D], U8, name="w1s", tag="w1s", align_bytes=64)
        w2q = keep.tile([P, KP, D], U32, name="w2q", tag="w2q", align_bytes=64)
        w2s = keep.tile([P, KP, D], U8, name="w2s", tag="w2s", align_bytes=64)
        fb = keep.tile([P, D], BF16, name="fb", tag="fb")
        gs = keep.tile([P, H], BF16, name="gs", tag="gs")
        bs = keep.tile([P, H], BF16, name="bs", tag="bs")
        g_raw = keep.tile([P, 16], BF16, name="g_raw", tag="g_raw")
        b_raw = keep.tile([P, 16], BF16, name="b_raw", tag="b_raw")
        g_col = keep.tile([P, 16], F32, name="g_col", tag="g_col")
        b_col = keep.tile([P, 16], F32, name="b_col", tag="b_col")

        def tok(i):
            return i // (T // P), (i % (T // P)) * P

        def new_grp():
            grp = work.tile([P, D], BF16, name="grp", tag="grp", bufs=3, align_bytes=64)
            return grp

        def word_transposes(words_of, h):
            bank = psum.tile([P, 512], F32, name="bank", tag="bank")
            for g2 in range(2):
                for u in range(2):
                    c0 = (2 * g2 + u) * P
                    nc.tensor.transpose(bank[:, c0:c0 + P], words_of(2 * h + g2, u), ident[:])
            return bank

        def word_evac(on_scalar, grp, bank, h):
            dst = grp[:].bitcast(F32).rearrange("p (g r u) -> p g r u", g=KP, r=P, u=2)[:, 2 * h:2 * h + 2]
            src = bank[:].rearrange("p (g u r) -> p g r u", g=2, u=2, r=P)
            if on_scalar:
                nc.scalar.copy(out=dst, in_=src)
            else:
                nc.vector.tensor_copy(out=dst, in_=src)

        w1_rows = wout_w.rearrange("(g p t) k -> g t p k", g=4, p=P, t=4)
        w_rows = []
        for u in range(2):
            for g in range(2):
                for e in range(2):
                    w_rows.append(w1_rows[g, 2 * u + e])
        w_cols = {}
        for tp in range(2):
            for t2 in range(2):
                for g2 in range(2):
                    w_cols[len(w_rows)] = (w1q, w1s, H + 256 * (2 * tp + t2) + P * g2)
                    w_rows.append(w1_rows[2 + g2, 2 * tp + t2])
        for rt in range(16):
            w_cols[len(w_rows)] = (w2q, w2s, rt * P)
            w_rows.append(ff1_w[rt * P:(rt + 1) * P, :])
        NPAIR = 8
        w_raw = {}
        w_grp = {}

        w_count = [0]

        def w_load(depth=7):
            for unused in range(depth):
                n = w_count[0]
                if len(w_raw) < depth and n < len(w_rows):
                    if n % 7 < 4:
                        raw = work.tile([P, D], BF16, name="raw", tag="raw", bufs=4)
                    else:
                        raw = work.tile([P, D], BF16, name="o", tag="o", bufs=3)
                    if n > 1:
                        nc.sync.dma_start(out=raw[:], in_=w_rows[n])
                    w_raw[n] = raw
                    w_count[0] += 1
                    if n == 1:
                        for k_lo in (0, H):
                            for n01 in range(2):
                                nc.sync.dma_start(out=w_raw[n01][:, k_lo:k_lo + H], in_=w_rows[n01][:, k_lo:k_lo + H])

        def w_transpose(n):
            grp = new_grp()
            if n < NPAIR:
                h = n % 2
                pair = (w_raw[n - h][:].bitcast(F32), w_raw[n - h + 1][:].bitcast(F32))
                for k2 in range(2):
                    kp = 2 * h + k2
                    bank = psum.tile([P, 512], F32, name="bank", tag="bank")
                    for e in range(2):
                        for u in range(2):
                            c0 = (2 * e + u) * P
                            nc.tensor.transpose(bank[:, c0:c0 + P], pair[e][:, 256 * kp + u:256 * (kp + 1):2],
                                                ident[:])
                    dst = grp[:].bitcast(F32).rearrange("p (k w e u) -> p k w e u", k=2, w=P, e=2, u=2)[:, k2]
                    src = bank[:].rearrange("p (e u w) -> p w e u", e=2, u=2, w=P)
                    if k2 == 0 or n % 2 == 1:
                        nc.scalar.copy(out=dst, in_=src)
                    else:
                        nc.vector.tensor_copy(out=dst, in_=src)
                if h == 1:
                    w_raw.pop(n - 1)
                    w_raw.pop(n)
            else:
                raw_w = w_raw.pop(n)[:].bitcast(F32)
                for h in range(2):
                    bank = word_transposes(lambda g, u: raw_w[:, 256 * g + u:256 * (g + 1):2], h)
                    word_evac(h == 0 or n % 2 == 1, grp, bank, h)
            w_grp[n] = grp

        def w_quantize(n):
            grp = w_grp.pop(n)
            if n < NPAIR:
                q4 = n // 2
                col0 = 512 * (q4 // 2) + 256 * (q4 % 2)
                for k2 in range(2):
                    kp = 2 * (n % 2) + k2
                    nc.vector.quantize_mx(out=w1q[:, kp, col0:col0 + 256].bitcast(FP8X4),
                                          scales=w1s[:, kp, col0:col0 + 256],
                                          in_=grp[:, 1024 * k2:1024 * (k2 + 1)])
            else:
                wq, ws, col0 = w_cols[n]
                for kp in range(KP):
                    nc.vector.quantize_mx(out=wq[:, kp, col0:col0 + P].bitcast(FP8X4),
                                          scales=ws[:, kp, col0:col0 + P],
                                          in_=grp[:, 512 * kp:512 * (kp + 1)])

        raws = {}
        srts = {}
        xs = {}
        axg = {}
        axb = {}
        axqs = {}
        rs = {}
        sums_d = {}
        stat = {}
        zs = {}
        mts = {}
        mgrp = {}
        mqs = {}
        os_d = {}

        def load_ax(i):
            if i < NT:
                s, t0 = tok(i)
                raw = work.tile([P, D], BF16, name="axraw", tag="axraw", bufs=3)
                nc.sync.dma_start(out=raw[:], in_=ax_cat[s, t0:t0 + P, :])
                raws[i] = raw

        def load_x(i):
            if i < NT:
                s, t0 = tok(i)
                x = work.tile([P, D], BF16, name="x", tag="x", bufs=3)
                nc.sync.dma_start(out=x[:], in_=features[0, t0:t0 + P, s, :])
                xs[i] = x

        def sort_ax(i):
            if i < NT:
                raw = raws.pop(i)
                srt = work.tile([P, D], BF16, name="srt", tag="srt", bufs=2)
                nc.scalar.copy(out=srt[:].bitcast(F32).rearrange("p (g u w) -> p g u w", g=KP, u=2, w=P),
                               in_=raw[:].bitcast(F32).rearrange("p (g w u) -> p g u w", g=KP, w=P, u=2))
                srts[i] = srt

        def ax_transposes(i):
            axg[i] = new_grp()
            axb[i] = []
            if i in srts:
                srt_w = srts.pop(i)[:].bitcast(F32)
                for h in range(2):
                    axb[i].append(word_transposes(lambda g, u: srt_w[:, (2 * g + u) * P:(2 * g + u + 1) * P], h))
            else:
                raw_w = raws.pop(i)[:].bitcast(F32)
                for h in range(2):
                    axb[i].append(word_transposes(lambda g, u: raw_w[:, 256 * g + u:256 * (g + 1):2], h))

        def ax_evac(i, h):
            word_evac(True, axg[i], axb[i][h], h)

        def ax_quantize(i):
            grp = axg.pop(i)
            axb.pop(i)
            q = work.tile([P, KP * P], U32, name="axq", tag="axq", bufs=2, align_bytes=64)
            sc = work.tile([P, KP * P], U8, name="axs", tag="axs", bufs=2, align_bytes=64)
            nc.vector.quantize_mx(out=q[:].bitcast(FP8X4), scales=sc[:], in_=grp[:])
            axqs[i] = (q, sc)

        def mx_group(q, sc, wq, ws, b):
            ps = psum.tile([P, 512], F32, name="bank", tag="bank")
            for kp in range(KP):
                nc.tensor.matmul_mx(out=ps[:],
                                    lhsT=q[:, kp * P:(kp + 1) * P].bitcast(FP8X4),
                                    lhsT_scale=sc[:, kp * P:(kp + 1) * P],
                                    rhs=wq[:, kp, 512 * b:512 * (b + 1)].bitcast(FP8X4),
                                    rhs_scale=ws[:, kp, 512 * b:512 * (b + 1)],
                                    start=(kp == 0), stop=(kp == KP - 1))
            return ps

        def stage1_bank(i, t):
            if t == 0:
                r_new = work.tile([P, D], F32, name="r", tag="r", bufs=2)
                sums_new = small.tile([P, NB], F32, name="sums", tag="sums")
                rs[i] = r_new
                sums_d[i] = sums_new
            q, sc = axqs[i]
            ps = mx_group(q, sc, w1q, w1s, t)
            r_b = rs[i][:, 512 * t:512 * (t + 1)]
            if t < 2:
                nc.vector.scalar_tensor_tensor(out=r_b.rearrange("p (v e) -> p v e", e=2),
                                               in0=ps[:].rearrange("p (v e) -> p v e", e=2), scalar=0.0,
                                               in1=xs[i][:, 0:H].rearrange("p (v u e) -> p u v e", u=2, e=2)[:, t],
                                               op0=ALU.add, op1=ALU.add, accum_out=sums_d[i][:, t:t + 1])
            else:
                c_lo = 2 * (t - 2)
                nc.vector.scalar_tensor_tensor(out=r_b.rearrange("p (c v) -> p c v", c=2),
                                               in0=ps[:].rearrange("p (c v) -> p c v", c=2), scalar=0.0,
                                               in1=xs[i][:, H:D].rearrange("p (v c) -> p c v", c=4)[:, c_lo:c_lo + 2],
                                               op0=ALU.add, op1=ALU.add, accum_out=sums_d[i][:, t:t + 1])
            if t == NB - 1:
                axqs.pop(i)
                xs.pop(i)

        def stats(i):
            r = rs[i]
            sums = sums_d.pop(i)
            junk4 = small.tile([P, NB], F32, name="junk4", tag="junk4")
            negmu = small.tile([P, 1], F32, name="negmu", tag="negmu")
            nc.scalar.activation(out=junk4[:], in_=sums[:], func=ACT.Copy, scale=-1.0 / D, accum_out=negmu[:])
            junk = work.tile([P, D], BF16, name="junk", tag="junk", bufs=1)
            ssq = small.tile([P, 1], F32, name="ssq", tag="ssq")
            nc.scalar.activation(out=junk[:], in_=r[:], func=ACT.Square, bias=negmu[:], scale=1.0,
                                 accum_out=ssq[:])
            std = small.tile([P, 1], F32, name="std", tag="std")
            nc.scalar.activation(out=std[:], in_=ssq[:], func=ACT.Sqrt, bias=eps_t[:], scale=1.0 / D)
            stat[i] = (negmu, std)

        us = {}
        m1s = {}

        def apply_start(i):
            negmu, std = stat[i]
            rstd = small.tile([P, 1], F32, name="rstd", tag="rstd")
            nc.vector.reciprocal(out=rstd[:], in_=std[:])
            stat[i] = (negmu, rstd)

        def apply_z(i):
            negmu, rstd = stat[i]
            z_new = work.tile([P, H], F32, name="z", tag="z", bufs=2)
            zs[i] = z_new
            nc.vector.tensor_scalar(out=z_new[:], in0=rs[i][:, H:D], scalar1=negmu[:], scalar2=rstd[:],
                                    op0=ALU.add, op1=ALU.mult)

        def apply_u(i):
            negmu, rstd = stat[i]
            u_new = work.tile([P, H], F32, name="u", tag="u", bufs=1)
            us[i] = u_new
            nc.vector.scalar_tensor_tensor(out=u_new[:], in0=rs[i][:, 0:H], scalar=negmu[:], in1=gs[:],
                                           op0=ALU.add, op1=ALU.mult)
            rs.pop(i)

        def apply_m(i, h):
            negmu, rstd = stat[i]
            if h == 0:
                m1_new = work.tile([P, H], BF16, name="m1", tag="m1", bufs=2)
                m1s[i] = m1_new
            lo, hi = 512 * h, 512 * (h + 1)
            nc.vector.scalar_tensor_tensor(out=m1s[i][:, lo:hi], in0=us[i][:, lo:hi], scalar=rstd[:],
                                           in1=bs[:, lo:hi], op0=ALU.mult, op1=ALU.add)
            if h == 1:
                us.pop(i)
                stat.pop(i)

        zb = {}

        def m_transposes(i):
            m1_w = m1s.pop(i)[:].bitcast(F32)
            zb[(i, 0)] = word_transposes(lambda g, u: m1_w[:, 256 * u + P * g:256 * u + P * (g + 1)], 0)
            z = zs.pop(i)
            for g2 in range(2):
                bank = psum.tile([P, 512], F32, name="bank", tag="bank")
                for t in range(4):
                    nc.tensor.transpose(bank[:, t * P:(t + 1) * P],
                                        z[:, 256 * t + P * g2:256 * t + P * (g2 + 1)], ident[:])
                zb[(i, 1 + g2)] = bank

        def m_evac(i):
            mgrp[i] = new_grp()
            word_evac(True, mgrp[i], zb.pop((i, 0)), 0)
            mt_new = work.tile([P, H], BF16, name="mt", tag="mt", bufs=2)
            mts[i] = mt_new
            for g2 in range(2):
                bank = zb.pop((i, 1 + g2))
                for t in range(4):
                    c = 4 * g2 + t
                    nc.scalar.activation(out=mt_new[:, c * P:(c + 1) * P], in_=bank[:, t * P:(t + 1) * P],
                                         func=ACT.Identity, scale=g_col[:, 8 + c:9 + c], bias=b_col[:, 8 + c:9 + c])

        def m_interleave(i):
            nc.vector.tensor_copy(out=mgrp[i][:, H:D].rearrange("p (g c t) -> p g c t", g=2, c=P, t=4),
                                  in_=mts.pop(i)[:].rearrange("p (g t c) -> p g c t", g=2, t=4, c=P))

        def m_quantize(i):
            grp = mgrp.pop(i)
            q = work.tile([P, KP * P], U32, name="mq", tag="mq", bufs=3, align_bytes=64)
            sc = work.tile([P, KP * P], U8, name="ms", tag="ms", bufs=3, align_bytes=64)
            nc.vector.quantize_mx(out=q[:].bitcast(FP8X4), scales=sc[:], in_=grp[:])
            mqs[i] = (q, sc)

        ovs = {}

        def stage2_bank(i, b):
            if b == 0:
                o_new = work.tile([P, D], F32, name="o", tag="o", bufs=3)
                os_d[i] = o_new
            q, sc = mqs[i]
            ps = mx_group(q, sc, w2q, w2s, b)
            if 512 * b >= VR and i < NT - 1:
                if 512 * b == VR:
                    ov_new = work.tile([P, D - VR], F32, name="ov", tag="ov", bufs=2)
                    ovs[i] = ov_new
                dst = ovs[i][:, 512 * b - VR:512 * (b + 1) - VR]
            else:
                dst = os_d[i][:, 512 * b:512 * (b + 1)]
            nc.vector.tensor_tensor(out=dst, in0=ps[:], in1=fb[:, 512 * b:512 * (b + 1)], op=ALU.add)
            if b == NB - 1:
                mqs.pop(i)

        def relu_store(i, lo, hi):
            s, t0 = tok(i)
            o = os_d[i]
            nc.scalar.activation(out=o[:, lo:hi], in_=o[:, lo:hi], func=ACT.Relu)
            nc.sync.dma_start(out=out[s, t0:t0 + P, lo:hi], in_=o[:, lo:hi])
            if hi == D:
                os_d.pop(i)

        def relu_store_shared(i):
            s, t0 = tok(i)
            o = os_d.pop(i)
            nc.vector.tensor_scalar_max(out=o[:, VR:D], in0=ovs.pop(i)[:], scalar1=0.0)
            nc.scalar.activation(out=o[:, 0:VR], in_=o[:, 0:VR], func=ACT.Relu)
            nc.sync.dma_start(out=out[s, t0:t0 + P, :], in_=o[:])

        w_load(2)
        nc.sync.dma_start(out=rowt[0:1, 0:H], in_=ln_g[0:H].rearrange("(o c) -> o c", o=1))
        nc.sync.dma_start(out=rowt[0:1, H:D], in_=ln_b[0:H].rearrange("(o c) -> o c", o=1))
        load_ax(0)
        w_load()
        for n in range(16):
            w_transpose(n)
            w_load()
            if n == 1:
                ax_transposes(0)
                ax_evac(0, 0)
                ax_evac(0, 1)
            if n == 3:
                for k in range(4):
                    bank = psum.tile([P, 512], F32, name="bank", tag="bank")
                    nc.tensor.matmul(out=bank[:], lhsT=ones[:], rhs=rowt[:, 512 * k:512 * (k + 1)], start=True, stop=True)
                    spread = (gs, bs)[k // 2]
                    v_lo = P * (k % 2)
                    nc.scalar.copy(out=spread[:].rearrange("p (u v e) -> p u v e", u=2, e=2)[:, :, v_lo:v_lo + P, :],
                                   in_=bank[:].rearrange("p (v u e) -> p u v e", u=2, e=2))
            if n == 2:
                load_x(0)
            if n == 5:
                load_ax(1)
            if n == 8:
                sort_ax(1)
            if n == 9:
                ax_transposes(1)
                ax_evac(1, 0)
                ax_evac(1, 1)
            if n > 0:
                w_quantize(n - 1)
            if n == 2:
                ax_quantize(0)
            if n == 10:
                ax_quantize(1)
            if n == 11:
                load_ax(2)
                load_x(1)
            if n == 14:
                sort_ax(2)
            if n > 3 and n % 4 == 0:
                stage1_bank(0, n // 4 - 1)
        load_ax(3)
        load_x(2)
        nc.sync.dma_start(out=g_raw[:].rearrange("p (g t) -> p g t", g=4, t=4),
                          in_=ln_g.rearrange("(g p t) -> p g t", g=4, p=P, t=4))
        nc.sync.dma_start(out=b_raw[:].rearrange("p (g t) -> p g t", g=4, t=4),
                          in_=ln_b.rearrange("(g p t) -> p g t", g=4, p=P, t=4))
        w_quantize(15)
        w_next = 16

        carried = []
        quantized = {}
        for j in range(1, NT + L2):
            i1, iz, i2 = j, j - LZ, j - L2
            has1 = i1 < NT
            hasz = 0 <= iz < NT
            has2 = 0 <= i2 < NT
            hasn = j - 1 < NT
            if j + 1 < NT:
                ax_transposes(j + 1)
            if hasz:
                m_transposes(iz)
            if j == 1:
                stage1_bank(0, 3)
            load_ax(j + 3)
            load_x(j + 2)
            if j + 1 < NT:
                ax_evac(j + 1, 0)
                ax_evac(j + 1, 1)
            late = j >= NT - 1
            if late and hasz:
                m_evac(iz)
            if hasn:
                stats(j - 1)
            for i_old in carried:
                relu_store_shared(i_old)
            carried = []
            if hasz and not late:
                m_evac(iz)
            sort_ax(j + 2)
            if 0 <= iz - 1 < NT and (iz - 1) not in quantized:
                m_interleave(iz - 1)
            if has1:
                stage1_bank(i1, 0)
            if 0 <= iz - 1 < NT and (iz - 1) not in quantized:
                m_quantize(iz - 1)
            if has1:
                stage1_bank(i1, 1)
            if j + 1 < NT:
                ax_quantize(j + 1)
            if has1:
                stage1_bank(i1, 2)
            if late and has1:
                m_interleave(iz)
            if has1:
                stage1_bank(i1, 3)
            if late and has1:
                m_quantize(iz)
                quantized[iz] = True
            if hasn and has1:
                apply_start(j - 1)
                apply_z(j - 1)
                apply_u(j - 1)
            if j == 1:
                nc.vector.tensor_copy(out=g_col[:], in_=g_raw[:])
                nc.vector.tensor_copy(out=b_col[:], in_=b_raw[:])
            if j < len(W2_SPLIT):
                for n_unit in range(W2_SPLIT[j]):
                    w_transpose(w_next)
                    w_load()
                    if n_unit < 2:
                        apply_m(j - 1, n_unit)
                    if n_unit > 0:
                        w_quantize(w_next - 1)
                    w_next += 1
                w_quantize(w_next - 1)
                if j == 2:
                    nc.sync.dma_start(out=fb[:], in_=ff1_b.partition_broadcast(P))
            elif has2:
                if i2 < NT - 1:
                    stage2_bank(i2, 0)
                    if hasn and has1:
                        apply_m(j - 1, 0)
                    stage2_bank(i2, 1)
                    if hasn and has1:
                        apply_m(j - 1, 1)
                    if hasz and not has1:
                        m_interleave(iz)
                    stage2_bank(i2, 2)
                    if hasz and not has1:
                        m_quantize(iz)
                        quantized[iz] = True
                    stage2_bank(i2, 3)
                    if hasn and not has1:
                        apply_start(j - 1)
                        apply_z(j - 1)
                        apply_u(j - 1)
                        apply_m(j - 1, 0)
                        apply_m(j - 1, 1)
                    carried.append(i2)
                else:
                    for b in range(NB):
                        stage2_bank(i2, b)
                        relu_store(i2, 512 * b, 512 * (b + 1))
